import numpy as np
import ml_dtypes


def mxq(x, axis, fmt="e4m3"):
    dtype, down = {"e4m3": (ml_dtypes.float8_e4m3fn, 7), "e5m2": (ml_dtypes.float8_e5m2, 14)}[fmt]
    v = np.moveaxis(np.asarray(x, np.float32).astype(ml_dtypes.bfloat16).astype(np.float64), axis, -1)
    blocks = v.reshape(v.shape[:-1] + (-1, 32))
    amax = np.abs(blocks).max(-1, keepdims=True)
    byte = np.maximum(np.where(amax > 0, np.frexp(amax)[1] - 1 + 127, 0) - down, 1)
    scale = np.exp2(byte - 127.0)
    codes = (blocks / scale).astype(np.float32).astype(dtype).astype(np.float64)
    return np.moveaxis((codes * scale).reshape(v.shape), -1, axis)


WIDE = False


def mx_kscale(k):
    if not WIDE:
        return np.ones(k)
    levels = np.array([10, -10, 5, -5, 0])
    a = np.random.permutation(np.resize(levels, k // 512 * 4)).reshape(k // 512, 4)
    idx = np.arange(k)
    return np.exp2(a[idx // 512, idx % 128 // 32])


BF16 = ml_dtypes.bfloat16


def bf(x):
    return np.asarray(x, np.float32).astype(BF16)


def f64(x):
    return np.asarray(x).astype(np.float64)


E2M1 = np.array([0.0, 0.5, 1.0, 1.5, 2.0, 3.0, 4.0, 6.0, -0.0, -0.5, -1.0, -1.5, -2.0, -3.0, -4.0, -6.0])


def pack_weight(w, fmt):
    k, n = w.shape
    w = f64(bf(w)).reshape(k // 32, 32, n)
    amax = np.abs(w).max(1)
    if fmt == "e4m3":
        byte = np.frexp(amax)[1] - 1 + 127 - 7
    else:
        mant, ex = np.frexp(amax / 6.0)
        byte = np.where(mant > 0.5, ex, ex - 1) + 127
    byte = np.clip(np.where(amax > 0, byte, 1), 1, 254)
    scaled = (w * np.exp2(127.0 - byte)[:, None, :]).reshape(k, n).astype(np.float32)
    by_word = np.ascontiguousarray(scaled.reshape(k // 512, 128, 4, n).transpose(0, 1, 3, 2))
    if fmt == "e4m3":
        words = by_word.astype(ml_dtypes.float8_e4m3fn).view(np.uint8)
    else:
        c = by_word.astype(ml_dtypes.float4_e2m1fn).view(np.uint8) & 0xF
        words = c[..., 0::2] | (c[..., 1::2] << 4)
    return np.ascontiguousarray(words), np.ascontiguousarray(byte.astype(np.uint8).reshape(k // 512, 16, n))


def unpack_weight(words, scales, fmt):
    g, p, n, _ = words.shape
    if fmt == "e4m3":
        vals = np.ascontiguousarray(words).view(ml_dtypes.float8_e4m3fn).astype(np.float64)
    else:
        nib = np.empty((g, p, n, 4), np.uint8)
        nib[..., 0::2] = words & 0xF
        nib[..., 1::2] = words >> 4
        vals = E2M1[nib]
    vals = vals * np.repeat(np.exp2(scales.astype(np.float64) - 127.0), 8, axis=1)[..., None]
    return vals.transpose(0, 1, 3, 2).reshape(g * 512, n)


B, T, D, H, HKV, HD, R, DFF = 2, 2048, 512, 4, 2, 128, 128, 6144
HALF = HD // 2
EPS = 1e-6
THETA = 1e6
FMT = "e4m3"


def rms_norm(x, w):
    return x / np.sqrt(np.mean(x * x, axis=-1, keepdims=True) + EPS) * w


def rotate_half(x):
    return np.concatenate([-x[..., HALF:], x[..., :HALF]], axis=-1)


def setup_inputs():
    rn = np.random.standard_normal
    s = mx_kscale(D)
    inv_freq = 1.0 / THETA ** (np.arange(HALF) / HALF)
    freqs = np.arange(T)[:, None] * inv_freq[None, :]
    emb = np.concatenate([freqs, freqs], axis=-1)
    hidden_states = bf(rn((B, T, D)) * np.exp(0.5 * rn((B, T, 1))))
    ln1_w = bf((1.0 + 0.1 * rn(D)) * s)
    Wq_words, Wq_scales = pack_weight(rn((D, H * HD)) / np.sqrt(D) / s[:, None], FMT)
    Wk_words, Wk_scales = pack_weight(rn((D, HKV * HD)) / np.sqrt(D) / s[:, None], FMT)
    Wv_words, Wv_scales = pack_weight(rn((D, HKV * HD)) / np.sqrt(D) / s[:, None], FMT)
    q_norm_w = bf(1.0 + 0.1 * rn(HD))
    k_norm_w = bf(1.0 + 0.1 * rn(HD))
    return {
        "hidden_states": hidden_states,
        "ln1_w": ln1_w,
        "Wq_words": Wq_words,
        "Wq_scales": Wq_scales,
        "Wk_words": Wk_words,
        "Wk_scales": Wk_scales,
        "Wv_words": Wv_words,
        "Wv_scales": Wv_scales,
        "q_norm_w": q_norm_w,
        "k_norm_w": k_norm_w,
        "cos": bf(np.cos(emb)),
        "sin": bf(np.sin(emb)),
    }


def reference(hidden_states, ln1_w, Wq_words, Wq_scales, Wk_words, Wk_scales, Wv_words, Wv_scales, q_norm_w, k_norm_w, cos, sin):
    h = rms_norm(f64(hidden_states), f64(ln1_w))
    hq = mxq(h, 2, "e4m3")
    q = rms_norm((hq @ unpack_weight(Wq_words, Wq_scales, FMT)).reshape(B, T, H, HD), f64(q_norm_w)).transpose(0, 2, 1, 3)
    k = rms_norm((hq @ unpack_weight(Wk_words, Wk_scales, FMT)).reshape(B, T, HKV, HD), f64(k_norm_w)).transpose(0, 2, 1, 3)
    v = (hq @ unpack_weight(Wv_words, Wv_scales, FMT)).reshape(B, T, HKV, HD).transpose(0, 2, 1, 3)
    c, s_ = f64(cos)[None, None], f64(sin)[None, None]
    q = q * c + rotate_half(q) * s_
    k = k * c + rotate_half(k) * s_
    return q, k, v

@@ -1,0 +1,281 @@
+from contextlib import ExitStack
+
+import concourse.mybir as mybir
+from concourse.masks import make_identity
+
+F32 = mybir.dt.float32
+BF16 = mybir.dt.bfloat16
+I32 = mybir.dt.int32
+U8 = mybir.dt.uint8
+U32 = mybir.dt.uint32
+FP8X4 = mybir.dt.float8_e4m3fn_x4
+ACT = mybir.ActivationFunctionType
+ALU = mybir.AluOpType
+
+P = 128
+BATCH = 2
+T = 2048
+D = 512
+HD = 128
+HALF = HD // 2
+Q_HEADS = 4
+K_HEADS = 2
+V_HEADS = 2
+ROPE_HEADS = Q_HEADS + K_HEADS
+J = T // P
+GROUP = 4
+TABLE_J = 2
+EPS = 1e-6
+SCALE_ROWS = 4
+
+FLOPS = 2 * BATCH * T * D * (Q_HEADS + K_HEADS + V_HEADS) * HD
+
+LAG_H = 1
+LAG_REGROUP = 2
+LAG_MATMUL = 3
+LAG_SQUARES = 4
+LAG_ROPE = 5
+
+
+def tile_rawkvinjector_pa_t_kernel(
+    tc,
+    hidden_states,
+    ln1_w,
+    Wq_words,
+    Wq_scales,
+    Wk_words,
+    Wk_scales,
+    Wv_words,
+    Wv_scales,
+    q_norm_w,
+    k_norm_w,
+    cos,
+    sin,
+    out_0,
+    out_1,
+    out_2,
+):
+    nc = tc.nc
+    with ExitStack() as ctx:
+        keep = ctx.enter_context(tc.tile_pool(name="keep", bufs=1))
+        small = ctx.enter_context(tc.tile_pool(name="small", bufs=4))
+        stage = ctx.enter_context(tc.tile_pool(name="stage", bufs=3))
+        psum_t = ctx.enter_context(tc.psum_pool(name="psum_t", bufs=2))
+        psum_u = ctx.enter_context(tc.psum_pool(name="psum_u", bufs=3))
+        ctx.enter_context(tc.manual_schedule())
+
+        x_sb = keep.tile([P, BATCH, J, D], BF16)
+        ln_w = keep.tile([P, D], BF16)
+        norm_w = keep.tile([P, 2, HD], BF16)
+        neg_w = keep.tile([P, 2, HALF], BF16)
+        cos_sb = keep.tile([P, J, HD], BF16)
+        sin_sb = keep.tile([P, J, HD], BF16)
+        tables = keep.tile([P, 2, J, 2, HD], F32)
+        ident = keep.tile([P, P], F32)
+        wq_words = keep.tile([P, Q_HEADS * HD], U32, align_bytes=64)
+        wkv_words = keep.tile([P, (K_HEADS + V_HEADS) * HD], U32, align_bytes=64)
+        wq_scales = keep.tile([P, Q_HEADS * HD], U8, align_bytes=64)
+        wkv_scales = keep.tile([P, (K_HEADS + V_HEADS) * HD], U8, align_bytes=64)
+
+        nc.vector.memset(wq_scales[:].bitcast(I32), 0)
+        nc.vector.memset(wkv_scales[:].bitcast(I32), 0)
+        make_identity(nc, ident[:])
+
+        x_dram = hidden_states.rearrange("b (p j) k -> p b j k", j=J)
+
+        def load_x(b, j0, j1):
+            nc.sync.dma_start(out=x_sb[:, b, j0:j1, :], in_=x_dram[:, b, j0:j1, :])
+
+        def load_scales(plane, cols, scales):
+            for quadrant in range(P // 32):
+                rows = slice(SCALE_ROWS * quadrant, SCALE_ROWS * (quadrant + 1))
+                parts = slice(32 * quadrant, 32 * quadrant + SCALE_ROWS)
+                nc.sync.dma_start(out=plane[parts, cols].bitcast(I32), in_=scales[0, rows, :].bitcast(I32))
+
+        def load_words(words, cols, packed):
+            nc.sync.dma_start(
+                out=words[:, cols].bitcast(I32),
+                in_=packed[0].rearrange("p n t -> p (n t)").bitcast(I32),
+            )
+
+        k_cols = slice(0, K_HEADS * HD)
+        v_cols = slice(K_HEADS * HD, (K_HEADS + V_HEADS) * HD)
+        nc.scalar.dma_start(out=ln_w[:], in_=ln1_w.partition_broadcast(P))
+        nc.scalar.dma_start(out=norm_w[:, 0, :], in_=q_norm_w.partition_broadcast(P))
+        nc.scalar.dma_start(out=norm_w[:, 1, :], in_=k_norm_w.partition_broadcast(P))
+        load_x(0, 0, GROUP // 2)
+        load_scales(wq_scales, slice(0, Q_HEADS * HD), Wq_scales)
+        load_scales(wkv_scales, k_cols, Wk_scales)
+        load_scales(wkv_scales, v_cols, Wv_scales)
+        load_words(wq_words, slice(0, Q_HEADS * HD), Wq_words)
+        load_words(wkv_words, k_cols, Wk_words)
+        load_words(wkv_words, v_cols, Wv_words)
+        load_x(0, GROUP // 2, GROUP)
+        nc.sync.dma_start(out=cos_sb[:], in_=cos.rearrange("(p j) d -> p j d", j=J))
+        nc.sync.dma_start(out=sin_sb[:], in_=sin.rearrange("(p j) d -> p j d", j=J))
+        load_x(1, 0, GROUP)
+        for j0 in range(GROUP, J, GROUP):
+            for b in range(BATCH):
+                load_x(b, j0, j0 + GROUP)
+
+        nc.gpsimd.tensor_scalar(
+            out=neg_w[:], in0=norm_w[:, :, HALF:HD], scalar1=-1.0, scalar2=0.0, op0=ALU.mult, op1=ALU.add
+        )
+
+        def build_tables(j0):
+            js = slice(j0, j0 + TABLE_J)
+            lo = slice(0, HALF)
+            hi = slice(HALF, HD)
+
+            def over_qk(trig):
+                return trig.unsqueeze(1).to_broadcast([P, 2, TABLE_J, trig.shape[2]])
+
+            def over_j(weight):
+                return weight.unsqueeze(2).to_broadcast([P, 2, TABLE_J, weight.shape[2]])
+
+            nc.gpsimd.tensor_tensor(
+                out=tables[:, :, js, 0, :], in0=over_qk(cos_sb[:, js, :]), in1=over_j(norm_w[:]), op=ALU.mult
+            )
+            nc.gpsimd.tensor_tensor(
+                out=tables[:, :, js, 1, lo], in0=over_qk(sin_sb[:, js, hi]), in1=over_j(norm_w[:, :, lo]), op=ALU.mult
+            )
+            nc.gpsimd.tensor_tensor(
+                out=tables[:, :, js, 1, hi], in0=over_qk(sin_sb[:, js, lo]), in1=over_j(neg_w[:]), op=ALU.mult
+            )
+
+        order = [(b, j0 + jj) for j0 in range(0, J, GROUP) for b in range(BATCH) for jj in range(GROUP)]
+        live = {}
+
+        def sum_x_squares(i):
+            b, j = order[i]
+            x_squares = stage.tile([P, D], BF16)
+            x_sum = small.tile([P, 1], F32)
+            x_std = small.tile([P, 1], F32)
+            nc.scalar.activation(out=x_squares[:], in_=x_sb[:, b, j, :], func=ACT.Square, accum_out=x_sum[:])
+            nc.scalar.activation(out=x_std[:], in_=x_sum[:], func=ACT.Sqrt, scale=1.0 / D, bias=EPS)
+            live["x_std", i] = x_std
+
+        def normalise_and_transpose(i):
+            b, j = order[i]
+            x_rstd = small.tile([P, 1], F32)
+            nc.vector.reciprocal(out=x_rstd[:], in_=live["x_std", i][:])
+            h = stage.tile([P, D], BF16)
+            nc.vector.scalar_tensor_tensor(
+                out=h[:], in0=x_sb[:, b, j, :], scalar=x_rstd[:], in1=ln_w[:], op0=ALU.mult, op1=ALU.mult
+            )
+            h_t = psum_t.tile([P, 2, P], F32)
+            h_words = h[:].bitcast(F32)
+            for u in range(2):
+                nc.tensor.transpose(h_t[:, u, :], h_words[:, u : D // 2 : 2], ident[:])
+            live["h_t", i] = h_t
+
+        def regroup(i):
+            h_t = live["h_t", i]
+            grouped = stage.tile([P, 4 * P], BF16, align_bytes=64)
+            nc.scalar.copy(
+                out=grouped[:].bitcast(F32).rearrange("p (r u) -> p r u", u=2),
+                in_=h_t[:].rearrange("p u r -> p r u"),
+            )
+            live["grouped", i] = grouped
+
+        def quantise_and_multiply(i):
+            grouped = live["grouped", i]
+            h_codes = stage.tile([P, P], U32, align_bytes=64)
+            h_scales = stage.tile([P, P], U8, align_bytes=64)
+            nc.vector.quantize_mx(out=h_codes[:].bitcast(FP8X4), scales=h_scales[:], in_=grouped[:])
+            u_q = psum_u.tile([P, Q_HEADS * HD], F32)
+            u_kv = psum_u.tile([P, (K_HEADS + V_HEADS) * HD], F32)
+            for product, words, scales in ((u_q, wq_words, wq_scales), (u_kv, wkv_words, wkv_scales)):
+                nc.tensor.matmul_mx(
+                    out=product[:],
+                    lhsT=h_codes[:].bitcast(FP8X4),
+                    lhsT_scale=h_scales[:],
+                    rhs=words[:].bitcast(FP8X4),
+                    rhs_scale=scales[:],
+                    start=True,
+                    stop=True,
+                )
+            live["u_q", i] = u_q
+            live["u_kv", i] = u_kv
+
+        def head_of(i, head):
+            if head < Q_HEADS:
+                return live["u_q", i][:, head * HD : (head + 1) * HD]
+            return live["u_kv", i][:, (head - Q_HEADS) * HD : (head - Q_HEADS + 1) * HD]
+
+        def copy_v_and_sum_squares(i):
+            jj = i % GROUP
+            if jj == 0:
+                o_v = stage.tile([P, V_HEADS, GROUP, HD], F32)
+                live["o_v", i // GROUP] = o_v
+            nc.scalar.copy(
+                out=live["o_v", i // GROUP][:, :, jj, :],
+                in_=live["u_kv", i][:, v_cols].rearrange("p (h d) -> p h d", h=V_HEADS),
+            )
+            u_squares = stage.tile([P, ROPE_HEADS, HD], BF16)
+            u_sum = small.tile([P, ROPE_HEADS], F32)
+            u_std = small.tile([P, ROPE_HEADS], F32)
+            for head in range(ROPE_HEADS):
+                nc.scalar.activation(
+                    out=u_squares[:, head, :],
+                    in_=head_of(i, head),
+                    func=ACT.Square,
+                    accum_out=u_sum[:, head : head + 1],
+                )
+            nc.scalar.activation(out=u_std[:], in_=u_sum[:], func=ACT.Sqrt, scale=1.0 / HD, bias=EPS)
+            live["u_std", i] = u_std
+
+        def rope_and_store(i):
+            b, j = order[i]
+            jj = i % GROUP
+            u_rstd = small.tile([P, ROPE_HEADS], F32)
+            nc.vector.reciprocal(out=u_rstd[:], in_=live["u_std", i][:])
+            products = stage.tile([P, ROPE_HEADS, 2, HD], F32)
+            for head in range(ROPE_HEADS):
+                q_or_k = 0 if head < Q_HEADS else 1
+                nc.vector.scalar_tensor_tensor(
+                    out=products[:, head, :, :],
+                    in0=head_of(i, head).unsqueeze(1).to_broadcast([P, 2, HD]),
+                    scalar=u_rstd[:, head : head + 1],
+                    in1=tables[:, q_or_k, j, :, :],
+                    op0=ALU.mult,
+                    op1=ALU.mult,
+                )
+            if jj == 0:
+                o_qk = stage.tile([P, ROPE_HEADS, GROUP, HD], F32)
+                live["o_qk", i // GROUP] = o_qk
+            o_qk = live["o_qk", i // GROUP]
+            for half in range(2):
+                here = slice(half * HALF, (half + 1) * HALF)
+                other = slice((1 - half) * HALF, (2 - half) * HALF)
+                nc.gpsimd.tensor_tensor(
+                    out=o_qk[:, :, jj, here], in0=products[:, :, 0, here], in1=products[:, :, 1, other], op=ALU.add
+                )
+            if jj == GROUP - 1:
+                js = slice(j - jj, j + 1)
+                o_v = live["o_v", i // GROUP]
+                for dram, sbuf in (
+                    (out_0, o_qk[:, 0:Q_HEADS, :, :]),
+                    (out_1, o_qk[:, Q_HEADS:ROPE_HEADS, :, :]),
+                    (out_2, o_v[:]),
+                ):
+                    nc.sync.dma_start(out=dram[b].rearrange("h (p j) d -> p h j d", j=J)[:, :, js, :], in_=sbuf)
+
+        for j0 in range(0, GROUP, TABLE_J):
+            build_tables(j0)
+        n = len(order)
+        for rnd in range(n + LAG_ROPE):
+            if rnd % (2 * TABLE_J) == 0 and GROUP + rnd // 2 < J:
+                build_tables(GROUP + rnd // 2)
+            if rnd < n:
+                sum_x_squares(rnd)
+            if 0 <= rnd - LAG_H < n:
+                normalise_and_transpose(rnd - LAG_H)
+            if 0 <= rnd - LAG_REGROUP < n:
+                regroup(rnd - LAG_REGROUP)
+            if 0 <= rnd - LAG_MATMUL < n:
+                quantise_and_multiply(rnd - LAG_MATMUL)
+            if 0 <= rnd - LAG_SQUARES < n:
+                copy_v_and_sum_squares(rnd - LAG_SQUARES)
+            if 0 <= rnd - LAG_ROPE < n:
+                rope_and_store(rnd - LAG_ROPE)

@@ -23,7 +23,8 @@ K_HEADS = 2
 V_HEADS = 2
 ROPE_HEADS = Q_HEADS + K_HEADS
 J = T // P
-GROUP = 4
+GROUP = 2
+X_LOAD = 4
 TABLE_J = 2
 EPS = 1e-6
 SCALE_ROWS = 4
@@ -35,6 +36,7 @@ LAG_REGROUP = 2
 LAG_MATMUL = 3
 LAG_SQUARES = 4
 LAG_ROPE = 5
+LAG_SUM = 6
 
 
 def tile_rawkvinjector_pa_t_kernel(
@@ -103,20 +105,25 @@ def tile_rawkvinjector_pa_t_kernel(
         nc.scalar.dma_start(out=ln_w[:], in_=ln1_w.partition_broadcast(P))
         nc.scalar.dma_start(out=norm_w[:, 0, :], in_=q_norm_w.partition_broadcast(P))
         nc.scalar.dma_start(out=norm_w[:, 1, :], in_=k_norm_w.partition_broadcast(P))
-        load_x(0, 0, GROUP // 2)
+        load_x(0, 0, GROUP)
         load_scales(wq_scales, slice(0, Q_HEADS * HD), Wq_scales)
         load_scales(wkv_scales, k_cols, Wk_scales)
         load_scales(wkv_scales, v_cols, Wv_scales)
         load_words(wq_words, slice(0, Q_HEADS * HD), Wq_words)
         load_words(wkv_words, k_cols, Wk_words)
         load_words(wkv_words, v_cols, Wv_words)
-        load_x(0, GROUP // 2, GROUP)
+        load_x(1, 0, GROUP)
         nc.sync.dma_start(out=cos_sb[:], in_=cos.rearrange("(p j) d -> p j d", j=J))
         nc.sync.dma_start(out=sin_sb[:], in_=sin.rearrange("(p j) d -> p j d", j=J))
-        load_x(1, 0, GROUP)
-        for j0 in range(GROUP, J, GROUP):
+        for b in range(BATCH):
+            load_x(b, GROUP, X_LOAD)
+        for j0 in range(X_LOAD, J, X_LOAD):
             for b in range(BATCH):
-                load_x(b, j0, j0 + GROUP)
+                load_x(b, j0, j0 + X_LOAD)
+
+        one = keep.tile([P, 1], F32)
+        nc.vector.memset(one[:], 1.0)
+        nc.scalar.activation(out=one[:], in_=one[:], func=ACT.Sqrt)
 
         nc.gpsimd.tensor_scalar(
             out=neg_w[:], in0=norm_w[:, :, HALF:HD], scalar1=-1.0, scalar2=0.0, op0=ALU.mult, op1=ALU.add
@@ -225,9 +232,8 @@ def tile_rawkvinjector_pa_t_kernel(
             nc.scalar.activation(out=u_std[:], in_=u_sum[:], func=ACT.Sqrt, scale=1.0 / HD, bias=EPS)
             live["u_std", i] = u_std
 
-        def rope_and_store(i):
+        def rope_products(i):
             b, j = order[i]
-            jj = i % GROUP
             u_rstd = small.tile([P, ROPE_HEADS], F32)
             nc.vector.reciprocal(out=u_rstd[:], in_=live["u_std", i][:])
             products = stage.tile([P, ROPE_HEADS, 2, HD], F32)
@@ -241,14 +247,20 @@ def tile_rawkvinjector_pa_t_kernel(
                     op0=ALU.mult,
                     op1=ALU.mult,
                 )
+            live["products", i] = products
+
+        def sum_and_store(i):
+            b, j = order[i]
+            jj = i % GROUP
+            products = live["products", i]
             if jj == 0:
                 o_qk = stage.tile([P, ROPE_HEADS, GROUP, HD], F32)
                 live["o_qk", i // GROUP] = o_qk
             o_qk = live["o_qk", i // GROUP]
-            for half in range(2):
+            for half, engine in ((0, nc.vector), (1, nc.gpsimd)):
                 here = slice(half * HALF, (half + 1) * HALF)
                 other = slice((1 - half) * HALF, (2 - half) * HALF)
-                nc.gpsimd.tensor_tensor(
+                engine.tensor_tensor(
                     out=o_qk[:, :, jj, here], in0=products[:, :, 0, here], in1=products[:, :, 1, other], op=ALU.add
                 )
             if jj == GROUP - 1:
@@ -261,12 +273,11 @@ def tile_rawkvinjector_pa_t_kernel(
                 ):
                     nc.sync.dma_start(out=dram[b].rearrange("h (p j) d -> p h j d", j=J)[:, :, js, :], in_=sbuf)
 
-        for j0 in range(0, GROUP, TABLE_J):
-            build_tables(j0)
+        build_tables(0)
         n = len(order)
-        for rnd in range(n + LAG_ROPE):
-            if rnd % (2 * TABLE_J) == 0 and GROUP + rnd // 2 < J:
-                build_tables(GROUP + rnd // 2)
+        for rnd in range(n + LAG_SUM):
+            if rnd % (BATCH * TABLE_J) == 0 and TABLE_J + rnd // BATCH < J:
+                build_tables(TABLE_J + rnd // BATCH)
             if rnd < n:
                 sum_x_squares(rnd)
             if 0 <= rnd - LAG_H < n:
@@ -278,4 +289,6 @@ def tile_rawkvinjector_pa_t_kernel(
             if 0 <= rnd - LAG_SQUARES < n:
                 copy_v_and_sum_squares(rnd - LAG_SQUARES)
             if 0 <= rnd - LAG_ROPE < n:
-                rope_and_store(rnd - LAG_ROPE)
+                rope_products(rnd - LAG_ROPE)
+            if 0 <= rnd - LAG_SUM < n:
+                sum_and_store(rnd - LAG_SUM)

@@ -23,9 +23,8 @@ K_HEADS = 2
 V_HEADS = 2
 ROPE_HEADS = Q_HEADS + K_HEADS
 J = T // P
-GROUP = 2
+PAIR = 2
 X_LOAD = 4
-TABLE_J = 2
 EPS = 1e-6
 SCALE_ROWS = 4
 
@@ -33,10 +32,10 @@ FLOPS = 2 * BATCH * T * D * (Q_HEADS + K_HEADS + V_HEADS) * HD
 
 LAG_H = 1
 LAG_REGROUP = 2
+LAG_QUANTISE = 3
 LAG_MATMUL = 3
 LAG_SQUARES = 4
 LAG_ROPE = 5
-LAG_SUM = 6
 
 
 def tile_rawkvinjector_pa_t_kernel(
@@ -62,25 +61,30 @@ def tile_rawkvinjector_pa_t_kernel(
         keep = ctx.enter_context(tc.tile_pool(name="keep", bufs=1))
         small = ctx.enter_context(tc.tile_pool(name="small", bufs=4))
         stage = ctx.enter_context(tc.tile_pool(name="stage", bufs=3))
-        psum_t = ctx.enter_context(tc.psum_pool(name="psum_t", bufs=2))
+        psum_w = ctx.enter_context(tc.psum_pool(name="psum_w", bufs=1))
+        psum_t = ctx.enter_context(tc.psum_pool(name="psum_t", bufs=1))
         psum_u = ctx.enter_context(tc.psum_pool(name="psum_u", bufs=3))
         ctx.enter_context(tc.manual_schedule())
 
         x_sb = keep.tile([P, BATCH, J, D], BF16)
-        ln_w = keep.tile([P, D], BF16)
+        ln_w_sb = keep.tile([P, D], BF16)
         norm_w = keep.tile([P, 2, HD], BF16)
         neg_w = keep.tile([P, 2, HALF], BF16)
         cos_sb = keep.tile([P, J, HD], BF16)
         sin_sb = keep.tile([P, J, HD], BF16)
         tables = keep.tile([P, 2, J, 2, HD], F32)
         ident = keep.tile([P, P], F32)
+        ident_bf = keep.tile([P, P], BF16)
         wq_words = keep.tile([P, Q_HEADS * HD], U32, align_bytes=64)
         wkv_words = keep.tile([P, (K_HEADS + V_HEADS) * HD], U32, align_bytes=64)
         wq_scales = keep.tile([P, Q_HEADS * HD], U8, align_bytes=64)
         wkv_scales = keep.tile([P, (K_HEADS + V_HEADS) * HD], U8, align_bytes=64)
+        one = keep.tile([P, 1], F32)
 
         nc.vector.memset(wq_scales[:].bitcast(I32), 0)
         nc.vector.memset(wkv_scales[:].bitcast(I32), 0)
+        nc.vector.memset(one[:], 1.0)
+        make_identity(nc, ident_bf[:])
         make_identity(nc, ident[:])
 
         x_dram = hidden_states.rearrange("b (p j) k -> p b j k", j=J)
@@ -102,43 +106,44 @@ def tile_rawkvinjector_pa_t_kernel(
 
         k_cols = slice(0, K_HEADS * HD)
         v_cols = slice(K_HEADS * HD, (K_HEADS + V_HEADS) * HD)
-        nc.scalar.dma_start(out=ln_w[:], in_=ln1_w.partition_broadcast(P))
+        nc.scalar.dma_start(out=ln_w_sb[:], in_=ln1_w.partition_broadcast(P))
         nc.scalar.dma_start(out=norm_w[:, 0, :], in_=q_norm_w.partition_broadcast(P))
         nc.scalar.dma_start(out=norm_w[:, 1, :], in_=k_norm_w.partition_broadcast(P))
-        load_x(0, 0, GROUP)
+        load_x(0, 0, PAIR)
         load_scales(wq_scales, slice(0, Q_HEADS * HD), Wq_scales)
         load_scales(wkv_scales, k_cols, Wk_scales)
         load_scales(wkv_scales, v_cols, Wv_scales)
         load_words(wq_words, slice(0, Q_HEADS * HD), Wq_words)
         load_words(wkv_words, k_cols, Wk_words)
         load_words(wkv_words, v_cols, Wv_words)
-        load_x(1, 0, GROUP)
+        load_x(1, 0, PAIR)
         nc.sync.dma_start(out=cos_sb[:], in_=cos.rearrange("(p j) d -> p j d", j=J))
         nc.sync.dma_start(out=sin_sb[:], in_=sin.rearrange("(p j) d -> p j d", j=J))
         for b in range(BATCH):
-            load_x(b, GROUP, X_LOAD)
+            load_x(b, PAIR, X_LOAD)
         for j0 in range(X_LOAD, J, X_LOAD):
             for b in range(BATCH):
                 load_x(b, j0, j0 + X_LOAD)
 
-        one = keep.tile([P, 1], F32)
-        nc.vector.memset(one[:], 1.0)
-        nc.scalar.activation(out=one[:], in_=one[:], func=ACT.Sqrt)
+        nc.scalar.activation(out=one[:], in_=one[:], func=ACT.Abs_reciprocal_sqrt)
+
+        ln_w = psum_w.tile([P, D], F32)
+        nc.tensor.matmul(out=ln_w[:], lhsT=ident_bf[:], rhs=ln_w_sb[:], start=True, stop=True)
 
         nc.gpsimd.tensor_scalar(
             out=neg_w[:], in0=norm_w[:, :, HALF:HD], scalar1=-1.0, scalar2=0.0, op0=ALU.mult, op1=ALU.add
         )
 
         def build_tables(j0):
-            js = slice(j0, j0 + TABLE_J)
+            js = slice(j0, j0 + PAIR)
             lo = slice(0, HALF)
             hi = slice(HALF, HD)
 
             def over_qk(trig):
-                return trig.unsqueeze(1).to_broadcast([P, 2, TABLE_J, trig.shape[2]])
+                return trig.unsqueeze(1).to_broadcast([P, 2, PAIR, trig.shape[2]])
 
             def over_j(weight):
-                return weight.unsqueeze(2).to_broadcast([P, 2, TABLE_J, weight.shape[2]])
+                return weight.unsqueeze(2).to_broadcast([P, 2, PAIR, weight.shape[2]])
 
             nc.gpsimd.tensor_tensor(
                 out=tables[:, :, js, 0, :], in0=over_qk(cos_sb[:, js, :]), in1=over_j(norm_w[:]), op=ALU.mult
@@ -150,53 +155,68 @@ def tile_rawkvinjector_pa_t_kernel(
                 out=tables[:, :, js, 1, hi], in0=over_qk(sin_sb[:, js, lo]), in1=over_j(neg_w[:]), op=ALU.mult
             )
 
-        order = [(b, j0 + jj) for j0 in range(0, J, GROUP) for b in range(BATCH) for jj in range(GROUP)]
+        pairs = [(b, j0) for j0 in range(0, J, PAIR) for b in range(BATCH)]
         live = {}
 
-        def sum_x_squares(i):
-            b, j = order[i]
-            x_squares = stage.tile([P, D], BF16)
-            x_sum = small.tile([P, 1], F32)
-            x_std = small.tile([P, 1], F32)
-            nc.scalar.activation(out=x_squares[:], in_=x_sb[:, b, j, :], func=ACT.Square, accum_out=x_sum[:])
-            nc.scalar.activation(out=x_std[:], in_=x_sum[:], func=ACT.Sqrt, scale=1.0 / D, bias=EPS)
-            live["x_std", i] = x_std
+        def sum_x_squares(n):
+            b, j0 = pairs[n]
+            x_squares = stage.tile([P, PAIR, D], BF16)
+            x_sum = small.tile([P, PAIR], F32)
+            x_rstd = small.tile([P, PAIR], F32)
+            for jj in range(PAIR):
+                nc.scalar.activation(
+                    out=x_squares[:, jj, :],
+                    in_=x_sb[:, b, j0 + jj, :],
+                    func=ACT.Square,
+                    accum_out=x_sum[:, jj : jj + 1],
+                )
+            nc.scalar.activation(out=x_rstd[:], in_=x_sum[:], func=ACT.Abs_reciprocal_sqrt, scale=1.0 / D, bias=EPS)
+            live["x_rstd", n] = x_rstd
 
-        def normalise_and_transpose(i):
-            b, j = order[i]
-            x_rstd = small.tile([P, 1], F32)
-            nc.vector.reciprocal(out=x_rstd[:], in_=live["x_std", i][:])
-            h = stage.tile([P, D], BF16)
-            nc.vector.scalar_tensor_tensor(
-                out=h[:], in0=x_sb[:, b, j, :], scalar=x_rstd[:], in1=ln_w[:], op0=ALU.mult, op1=ALU.mult
-            )
-            h_t = psum_t.tile([P, 2, P], F32)
-            h_words = h[:].bitcast(F32)
-            for u in range(2):
-                nc.tensor.transpose(h_t[:, u, :], h_words[:, u : D // 2 : 2], ident[:])
-            live["h_t", i] = h_t
+        def normalise_and_transpose(n):
+            b, j0 = pairs[n]
+            x_rstd = live["x_rstd", n]
+            h = stage.tile([P, PAIR, D], BF16)
+            for jj in range(PAIR):
+                nc.vector.scalar_tensor_tensor(
+                    out=h[:, jj, :],
+                    in0=x_sb[:, b, j0 + jj, :],
+                    scalar=x_rstd[:, jj : jj + 1],
+                    in1=ln_w[:],
+                    op0=ALU.mult,
+                    op1=ALU.mult,
+                )
+            h_t = psum_t.tile([P, 2, PAIR * P], F32)
+            for jj in range(PAIR):
+                h_words = h[:, jj, :].bitcast(F32)
+                for u in range(2):
+                    nc.tensor.transpose(h_t[:, u, jj * P : (jj + 1) * P], h_words[:, u : D // 2 : 2], ident[:])
+            live["h_t", n] = h_t
 
-        def regroup(i):
-            h_t = live["h_t", i]
-            grouped = stage.tile([P, 4 * P], BF16, align_bytes=64)
+        def regroup(n):
+            grouped = stage.tile([P, PAIR * P * 4], BF16, align_bytes=64)
             nc.scalar.copy(
                 out=grouped[:].bitcast(F32).rearrange("p (r u) -> p r u", u=2),
-                in_=h_t[:].rearrange("p u r -> p r u"),
+                in_=live["h_t", n][:].rearrange("p u r -> p r u"),
             )
-            live["grouped", i] = grouped
+            live["grouped", n] = grouped
 
-        def quantise_and_multiply(i):
-            grouped = live["grouped", i]
-            h_codes = stage.tile([P, P], U32, align_bytes=64)
-            h_scales = stage.tile([P, P], U8, align_bytes=64)
-            nc.vector.quantize_mx(out=h_codes[:].bitcast(FP8X4), scales=h_scales[:], in_=grouped[:])
+        def quantise(n):
+            h_codes = stage.tile([P, PAIR * P], U32, align_bytes=64)
+            h_scales = stage.tile([P, PAIR * P], U8, align_bytes=64)
+            nc.vector.quantize_mx(out=h_codes[:].bitcast(FP8X4), scales=h_scales[:], in_=live["grouped", n][:])
+            live["h_codes", n] = h_codes
+            live["h_scales", n] = h_scales
+
+        def multiply(i):
+            tokens = slice((i % PAIR) * P, (i % PAIR + 1) * P)
             u_q = psum_u.tile([P, Q_HEADS * HD], F32)
             u_kv = psum_u.tile([P, (K_HEADS + V_HEADS) * HD], F32)
             for product, words, scales in ((u_q, wq_words, wq_scales), (u_kv, wkv_words, wkv_scales)):
                 nc.tensor.matmul_mx(
                     out=product[:],
-                    lhsT=h_codes[:].bitcast(FP8X4),
-                    lhsT_scale=h_scales[:],
+                    lhsT=live["h_codes", i // PAIR][:, tokens].bitcast(FP8X4),
+                    lhsT_scale=live["h_scales", i // PAIR][:, tokens],
                     rhs=words[:].bitcast(FP8X4),
                     rhs_scale=scales[:],
                     start=True,
@@ -211,17 +231,17 @@ def tile_rawkvinjector_pa_t_kernel(
             return live["u_kv", i][:, (head - Q_HEADS) * HD : (head - Q_HEADS + 1) * HD]
 
         def copy_v_and_sum_squares(i):
-            jj = i % GROUP
+            jj = i % PAIR
             if jj == 0:
-                o_v = stage.tile([P, V_HEADS, GROUP, HD], F32)
-                live["o_v", i // GROUP] = o_v
+                o_v = stage.tile([P, V_HEADS, PAIR, HD], F32)
+                live["o_v", i // PAIR] = o_v
             nc.scalar.copy(
-                out=live["o_v", i // GROUP][:, :, jj, :],
+                out=live["o_v", i // PAIR][:, :, jj, :],
                 in_=live["u_kv", i][:, v_cols].rearrange("p (h d) -> p h d", h=V_HEADS),
             )
             u_squares = stage.tile([P, ROPE_HEADS, HD], BF16)
             u_sum = small.tile([P, ROPE_HEADS], F32)
-            u_std = small.tile([P, ROPE_HEADS], F32)
+            u_rstd = small.tile([P, ROPE_HEADS], F32)
             for head in range(ROPE_HEADS):
                 nc.scalar.activation(
                     out=u_squares[:, head, :],
@@ -229,13 +249,13 @@ def tile_rawkvinjector_pa_t_kernel(
                     func=ACT.Square,
                     accum_out=u_sum[:, head : head + 1],
                 )
-            nc.scalar.activation(out=u_std[:], in_=u_sum[:], func=ACT.Sqrt, scale=1.0 / HD, bias=EPS)
-            live["u_std", i] = u_std
+            nc.scalar.activation(out=u_rstd[:], in_=u_sum[:], func=ACT.Abs_reciprocal_sqrt, scale=1.0 / HD, bias=EPS)
+            live["u_rstd", i] = u_rstd
 
-        def rope_products(i):
-            b, j = order[i]
-            u_rstd = small.tile([P, ROPE_HEADS], F32)
-            nc.vector.reciprocal(out=u_rstd[:], in_=live["u_std", i][:])
+        def rope_and_store(i):
+            b, j0 = pairs[i // PAIR]
+            jj = i % PAIR
+            u_rstd = live["u_rstd", i]
             products = stage.tile([P, ROPE_HEADS, 2, HD], F32)
             for head in range(ROPE_HEADS):
                 q_or_k = 0 if head < Q_HEADS else 1
@@ -243,52 +263,50 @@ def tile_rawkvinjector_pa_t_kernel(
                     out=products[:, head, :, :],
                     in0=head_of(i, head).unsqueeze(1).to_broadcast([P, 2, HD]),
                     scalar=u_rstd[:, head : head + 1],
-                    in1=tables[:, q_or_k, j, :, :],
+                    in1=tables[:, q_or_k, j0 + jj, :, :],
                     op0=ALU.mult,
                     op1=ALU.mult,
                 )
-            live["products", i] = products
-
-        def sum_and_store(i):
-            b, j = order[i]
-            jj = i % GROUP
-            products = live["products", i]
             if jj == 0:
-                o_qk = stage.tile([P, ROPE_HEADS, GROUP, HD], F32)
-                live["o_qk", i // GROUP] = o_qk
-            o_qk = live["o_qk", i // GROUP]
-            for half, engine in ((0, nc.vector), (1, nc.gpsimd)):
+                o_qk = stage.tile([P, ROPE_HEADS, PAIR, HD], F32)
+                live["o_qk", i // PAIR] = o_qk
+            o_qk = live["o_qk", i // PAIR]
+            for half in range(2):
                 here = slice(half * HALF, (half + 1) * HALF)
                 other = slice((1 - half) * HALF, (2 - half) * HALF)
-                engine.tensor_tensor(
+                nc.gpsimd.tensor_tensor(
                     out=o_qk[:, :, jj, here], in0=products[:, :, 0, here], in1=products[:, :, 1, other], op=ALU.add
                 )
-            if jj == GROUP - 1:
-                js = slice(j - jj, j + 1)
-                o_v = live["o_v", i // GROUP]
+            if jj == PAIR - 1:
+                js = slice(j0, j0 + PAIR)
                 for dram, sbuf in (
                     (out_0, o_qk[:, 0:Q_HEADS, :, :]),
                     (out_1, o_qk[:, Q_HEADS:ROPE_HEADS, :, :]),
-                    (out_2, o_v[:]),
+                    (out_2, live["o_v", i // PAIR][:]),
                 ):
                     nc.sync.dma_start(out=dram[b].rearrange("h (p j) d -> p h j d", j=J)[:, :, js, :], in_=sbuf)
 
+        def pair_at(step, lag):
+            first = step - lag
+            if first % PAIR == 0 and 0 <= first // PAIR < len(pairs):
+                return first // PAIR
+            return None
+
+        def tile_at(step, lag):
+            return step - lag if 0 <= step - lag < PAIR * len(pairs) else None
+
+        def run(one_stage, index):
+            if index is not None:
+                one_stage(index)
+
         build_tables(0)
-        n = len(order)
-        for rnd in range(n + LAG_SUM):
-            if rnd % (BATCH * TABLE_J) == 0 and TABLE_J + rnd // BATCH < J:
-                build_tables(TABLE_J + rnd // BATCH)
-            if rnd < n:
-                sum_x_squares(rnd)
-            if 0 <= rnd - LAG_H < n:
-                normalise_and_transpose(rnd - LAG_H)
-            if 0 <= rnd - LAG_REGROUP < n:
-                regroup(rnd - LAG_REGROUP)
-            if 0 <= rnd - LAG_MATMUL < n:
-                quantise_and_multiply(rnd - LAG_MATMUL)
-            if 0 <= rnd - LAG_SQUARES < n:
-                copy_v_and_sum_squares(rnd - LAG_SQUARES)
-            if 0 <= rnd - LAG_ROPE < n:
-                rope_products(rnd - LAG_ROPE)
-            if 0 <= rnd - LAG_SUM < n:
-                sum_and_store(rnd - LAG_SUM)
+        for step in range(PAIR * len(pairs) + LAG_ROPE):
+            if step % (BATCH * PAIR) == 0 and PAIR + step // BATCH < J:
+                build_tables(PAIR + step // BATCH)
+            run(sum_x_squares, pair_at(step, 0))
+            run(normalise_and_transpose, pair_at(step, LAG_H))
+            run(regroup, pair_at(step, LAG_REGROUP))
+            run(quantise, pair_at(step, LAG_QUANTISE))
+            run(multiply, tile_at(step, LAG_MATMUL))
+            run(copy_v_and_sum_squares, tile_at(step, LAG_SQUARES))
+            run(rope_and_store, tile_at(step, LAG_ROPE))

@@ -25,6 +25,7 @@ ROPE_HEADS = Q_HEADS + K_HEADS
 J = T // P
 PAIR = 2
 X_LOAD = 4
+TABLE_J = 4
 EPS = 1e-6
 SCALE_ROWS = 4
 
@@ -109,7 +110,15 @@ def tile_rawkvinjector_pa_t_kernel(
         nc.scalar.dma_start(out=ln_w_sb[:], in_=ln1_w.partition_broadcast(P))
         nc.scalar.dma_start(out=norm_w[:, 0, :], in_=q_norm_w.partition_broadcast(P))
         nc.scalar.dma_start(out=norm_w[:, 1, :], in_=k_norm_w.partition_broadcast(P))
+        cos_dram = cos.rearrange("(p j) d -> p j d", j=J)
+        sin_dram = sin.rearrange("(p j) d -> p j d", j=J)
+
+        def load_cos_sin(j0, j1):
+            nc.sync.dma_start(out=cos_sb[:, j0:j1, :], in_=cos_dram[:, j0:j1, :])
+            nc.sync.dma_start(out=sin_sb[:, j0:j1, :], in_=sin_dram[:, j0:j1, :])
+
         load_x(0, 0, PAIR)
+        load_cos_sin(0, TABLE_J)
         load_scales(wq_scales, slice(0, Q_HEADS * HD), Wq_scales)
         load_scales(wkv_scales, k_cols, Wk_scales)
         load_scales(wkv_scales, v_cols, Wv_scales)
@@ -117,10 +126,9 @@ def tile_rawkvinjector_pa_t_kernel(
         load_words(wkv_words, k_cols, Wk_words)
         load_words(wkv_words, v_cols, Wv_words)
         load_x(1, 0, PAIR)
-        nc.sync.dma_start(out=cos_sb[:], in_=cos.rearrange("(p j) d -> p j d", j=J))
-        nc.sync.dma_start(out=sin_sb[:], in_=sin.rearrange("(p j) d -> p j d", j=J))
         for b in range(BATCH):
             load_x(b, PAIR, X_LOAD)
+        load_cos_sin(TABLE_J, J)
         for j0 in range(X_LOAD, J, X_LOAD):
             for b in range(BATCH):
                 load_x(b, j0, j0 + X_LOAD)
@@ -134,18 +142,18 @@ def tile_rawkvinjector_pa_t_kernel(
             out=neg_w[:], in0=norm_w[:, :, HALF:HD], scalar1=-1.0, scalar2=0.0, op0=ALU.mult, op1=ALU.add
         )
 
-        def build_tables(j0):
-            js = slice(j0, j0 + PAIR)
+        def build_tables(j0, cos_engine):
+            js = slice(j0, j0 + TABLE_J)
             lo = slice(0, HALF)
             hi = slice(HALF, HD)
 
             def over_qk(trig):
-                return trig.unsqueeze(1).to_broadcast([P, 2, PAIR, trig.shape[2]])
+                return trig.unsqueeze(1).to_broadcast([P, 2, TABLE_J, trig.shape[2]])
 
             def over_j(weight):
-                return weight.unsqueeze(2).to_broadcast([P, 2, PAIR, weight.shape[2]])
+                return weight.unsqueeze(2).to_broadcast([P, 2, TABLE_J, weight.shape[2]])
 
-            nc.gpsimd.tensor_tensor(
+            cos_engine.tensor_tensor(
                 out=tables[:, :, js, 0, :], in0=over_qk(cos_sb[:, js, :]), in1=over_j(norm_w[:]), op=ALU.mult
             )
             nc.gpsimd.tensor_tensor(
@@ -256,28 +264,31 @@ def tile_rawkvinjector_pa_t_kernel(
             b, j0 = pairs[i // PAIR]
             jj = i % PAIR
             u_rstd = live["u_rstd", i]
-            products = stage.tile([P, ROPE_HEADS, 2, HD], F32)
+            if jj == 0:
+                products = stage.tile([P, PAIR, ROPE_HEADS, 2, HD], F32)
+                live["products", i // PAIR] = products
+            products = live["products", i // PAIR]
             for head in range(ROPE_HEADS):
                 q_or_k = 0 if head < Q_HEADS else 1
                 nc.vector.scalar_tensor_tensor(
-                    out=products[:, head, :, :],
+                    out=products[:, jj, head, :, :],
                     in0=head_of(i, head).unsqueeze(1).to_broadcast([P, 2, HD]),
                     scalar=u_rstd[:, head : head + 1],
                     in1=tables[:, q_or_k, j0 + jj, :, :],
                     op0=ALU.mult,
                     op1=ALU.mult,
                 )
-            if jj == 0:
-                o_qk = stage.tile([P, ROPE_HEADS, PAIR, HD], F32)
-                live["o_qk", i // PAIR] = o_qk
-            o_qk = live["o_qk", i // PAIR]
-            for half in range(2):
-                here = slice(half * HALF, (half + 1) * HALF)
-                other = slice((1 - half) * HALF, (2 - half) * HALF)
-                nc.gpsimd.tensor_tensor(
-                    out=o_qk[:, :, jj, here], in0=products[:, :, 0, here], in1=products[:, :, 1, other], op=ALU.add
-                )
             if jj == PAIR - 1:
+                o_qk = stage.tile([P, ROPE_HEADS, PAIR, HD], F32)
+                for half in range(2):
+                    here = slice(half * HALF, (half + 1) * HALF)
+                    other = slice((1 - half) * HALF, (2 - half) * HALF)
+                    nc.gpsimd.tensor_tensor(
+                        out=o_qk[:, :, :, here].rearrange("p h j d -> p j h d"),
+                        in0=products[:, :, :, 0, here],
+                        in1=products[:, :, :, 1, other],
+                        op=ALU.add,
+                    )
                 js = slice(j0, j0 + PAIR)
                 for dram, sbuf in (
                     (out_0, o_qk[:, 0:Q_HEADS, :, :]),
@@ -299,14 +310,15 @@ def tile_rawkvinjector_pa_t_kernel(
             if index is not None:
                 one_stage(index)
 
-        build_tables(0)
+        table_steps = BATCH * TABLE_J
+        build_tables(0, nc.gpsimd)
         for step in range(PAIR * len(pairs) + LAG_ROPE):
-            if step % (BATCH * PAIR) == 0 and PAIR + step // BATCH < J:
-                build_tables(PAIR + step // BATCH)
             run(sum_x_squares, pair_at(step, 0))
+            run(quantise, pair_at(step, LAG_QUANTISE))
+            if step % table_steps == LAG_QUANTISE and (step // table_steps + 1) * TABLE_J < J:
+                build_tables((step // table_steps + 1) * TABLE_J, nc.vector)
+            run(multiply, tile_at(step, LAG_MATMUL))
             run(normalise_and_transpose, pair_at(step, LAG_H))
             run(regroup, pair_at(step, LAG_REGROUP))
-            run(quantise, pair_at(step, LAG_QUANTISE))
-            run(multiply, tile_at(step, LAG_MATMUL))
             run(copy_v_and_sum_squares, tile_at(step, LAG_SQUARES))
             run(rope_and_store, tile_at(step, LAG_ROPE))

@@ -33,10 +33,10 @@ FLOPS = 2 * BATCH * T * D * (Q_HEADS + K_HEADS + V_HEADS) * HD
 
 LAG_H = 1
 LAG_REGROUP = 2
-LAG_QUANTISE = 3
-LAG_MATMUL = 3
-LAG_SQUARES = 4
-LAG_ROPE = 5
+LAG_QUANTISE = 5
+LAG_MATMUL = 5
+LAG_SQUARES = 6
+LAG_ROPE = 7
 
 
 def tile_rawkvinjector_pa_t_kernel(
@@ -247,6 +247,12 @@ def tile_rawkvinjector_pa_t_kernel(
                 out=live["o_v", i // PAIR][:, :, jj, :],
                 in_=live["u_kv", i][:, v_cols].rearrange("p (h d) -> p h d", h=V_HEADS),
             )
+            if jj == PAIR - 1:
+                b, j0 = pairs[i // PAIR]
+                nc.sync.dma_start(
+                    out=out_2[b].rearrange("h (p j) d -> p h j d", j=J)[:, :, j0 : j0 + PAIR, :],
+                    in_=live["o_v", i // PAIR][:],
+                )
             u_squares = stage.tile([P, ROPE_HEADS, HD], BF16)
             u_sum = small.tile([P, ROPE_HEADS], F32)
             u_rstd = small.tile([P, ROPE_HEADS], F32)
@@ -278,24 +284,24 @@ def tile_rawkvinjector_pa_t_kernel(
                     op0=ALU.mult,
                     op1=ALU.mult,
                 )
-            if jj == PAIR - 1:
+            together = 1 if i // PAIR == len(pairs) - 1 else PAIR
+            if jj == 0:
                 o_qk = stage.tile([P, ROPE_HEADS, PAIR, HD], F32)
-                for half in range(2):
-                    here = slice(half * HALF, (half + 1) * HALF)
-                    other = slice((1 - half) * HALF, (2 - half) * HALF)
-                    nc.gpsimd.tensor_tensor(
-                        out=o_qk[:, :, :, here].rearrange("p h j d -> p j h d"),
-                        in0=products[:, :, :, 0, here],
-                        in1=products[:, :, :, 1, other],
-                        op=ALU.add,
+                live["o_qk", i // PAIR] = o_qk
+            o_qk = live["o_qk", i // PAIR]
+            if (jj + 1) % together == 0:
+                jjs = slice(jj + 1 - together, jj + 1)
+                nc.gpsimd.tensor_tensor(
+                    out=o_qk[:, :, jjs, :].rearrange("p h j (x d) -> p j h x d", x=2),
+                    in0=products[:, jjs, :, 0, :].rearrange("p j h (x d) -> p j h x d", x=2),
+                    in1=products[:, jjs, :, 1, :].rearrange("p j h (x d) -> p j h x d", x=2)[:, :, :, ::-1, :],
+                    op=ALU.add,
+                )
+                js = slice(j0 + jj + 1 - together, j0 + jj + 1)
+                for dram, heads in ((out_0, slice(0, Q_HEADS)), (out_1, slice(Q_HEADS, ROPE_HEADS))):
+                    nc.sync.dma_start(
+                        out=dram[b].rearrange("h (p j) d -> p h j d", j=J)[:, :, js, :], in_=o_qk[:, heads, jjs, :]
                     )
-                js = slice(j0, j0 + PAIR)
-                for dram, sbuf in (
-                    (out_0, o_qk[:, 0:Q_HEADS, :, :]),
-                    (out_1, o_qk[:, Q_HEADS:ROPE_HEADS, :, :]),
-                    (out_2, live["o_v", i // PAIR][:]),
-                ):
-                    nc.sync.dma_start(out=dram[b].rearrange("h (p j) d -> p h j d", j=J)[:, :, js, :], in_=sbuf)
 
         def pair_at(step, lag):
             first = step - lag

@@ -142,25 +142,17 @@ def tile_rawkvinjector_pa_t_kernel(
             out=neg_w[:], in0=norm_w[:, :, HALF:HD], scalar1=-1.0, scalar2=0.0, op0=ALU.mult, op1=ALU.add
         )
 
-        def build_tables(j0, cos_engine):
+        def build_table_part(j0, table, half):
             js = slice(j0, j0 + TABLE_J)
-            lo = slice(0, HALF)
-            hi = slice(HALF, HD)
-
-            def over_qk(trig):
-                return trig.unsqueeze(1).to_broadcast([P, 2, TABLE_J, trig.shape[2]])
-
-            def over_j(weight):
-                return weight.unsqueeze(2).to_broadcast([P, 2, TABLE_J, weight.shape[2]])
-
-            cos_engine.tensor_tensor(
-                out=tables[:, :, js, 0, :], in0=over_qk(cos_sb[:, js, :]), in1=over_j(norm_w[:]), op=ALU.mult
-            )
+            here = slice(half * HALF, (half + 1) * HALF)
+            other = slice((1 - half) * HALF, (2 - half) * HALF)
+            trig = cos_sb[:, js, here] if table == 0 else sin_sb[:, js, other]
+            weight = neg_w[:] if (table, half) == (1, 1) else norm_w[:, :, here]
             nc.gpsimd.tensor_tensor(
-                out=tables[:, :, js, 1, lo], in0=over_qk(sin_sb[:, js, hi]), in1=over_j(norm_w[:, :, lo]), op=ALU.mult
-            )
-            nc.gpsimd.tensor_tensor(
-                out=tables[:, :, js, 1, hi], in0=over_qk(sin_sb[:, js, lo]), in1=over_j(neg_w[:]), op=ALU.mult
+                out=tables[:, :, js, table, here],
+                in0=trig.unsqueeze(1).to_broadcast([P, 2, TABLE_J, HALF]),
+                in1=weight.unsqueeze(2).to_broadcast([P, 2, TABLE_J, HALF]),
+                op=ALU.mult,
             )
 
         pairs = [(b, j0) for j0 in range(0, J, PAIR) for b in range(BATCH)]
@@ -170,7 +162,6 @@ def tile_rawkvinjector_pa_t_kernel(
             b, j0 = pairs[n]
             x_squares = stage.tile([P, PAIR, D], BF16)
             x_sum = small.tile([P, PAIR], F32)
-            x_rstd = small.tile([P, PAIR], F32)
             for jj in range(PAIR):
                 nc.scalar.activation(
                     out=x_squares[:, jj, :],
@@ -178,7 +169,13 @@ def tile_rawkvinjector_pa_t_kernel(
                     func=ACT.Square,
                     accum_out=x_sum[:, jj : jj + 1],
                 )
-            nc.scalar.activation(out=x_rstd[:], in_=x_sum[:], func=ACT.Abs_reciprocal_sqrt, scale=1.0 / D, bias=EPS)
+            live["x_sum", n] = x_sum
+
+        def x_rsqrt(n):
+            x_rstd = small.tile([P, PAIR], F32)
+            nc.scalar.activation(
+                out=x_rstd[:], in_=live["x_sum", n][:], func=ACT.Abs_reciprocal_sqrt, scale=1.0 / D, bias=EPS
+            )
             live["x_rstd", n] = x_rstd
 
         def normalise_and_transpose(n):
@@ -238,21 +235,8 @@ def tile_rawkvinjector_pa_t_kernel(
                 return live["u_q", i][:, head * HD : (head + 1) * HD]
             return live["u_kv", i][:, (head - Q_HEADS) * HD : (head - Q_HEADS + 1) * HD]
 
-        def copy_v_and_sum_squares(i):
+        def sum_squares_and_copy_v(i):
             jj = i % PAIR
-            if jj == 0:
-                o_v = stage.tile([P, V_HEADS, PAIR, HD], F32)
-                live["o_v", i // PAIR] = o_v
-            nc.scalar.copy(
-                out=live["o_v", i // PAIR][:, :, jj, :],
-                in_=live["u_kv", i][:, v_cols].rearrange("p (h d) -> p h d", h=V_HEADS),
-            )
-            if jj == PAIR - 1:
-                b, j0 = pairs[i // PAIR]
-                nc.sync.dma_start(
-                    out=out_2[b].rearrange("h (p j) d -> p h j d", j=J)[:, :, j0 : j0 + PAIR, :],
-                    in_=live["o_v", i // PAIR][:],
-                )
             u_squares = stage.tile([P, ROPE_HEADS, HD], BF16)
             u_sum = small.tile([P, ROPE_HEADS], F32)
             u_rstd = small.tile([P, ROPE_HEADS], F32)
@@ -263,8 +247,18 @@ def tile_rawkvinjector_pa_t_kernel(
                     func=ACT.Square,
                     accum_out=u_sum[:, head : head + 1],
                 )
+            if jj == 0:
+                o_v = stage.tile([P, V_HEADS, PAIR, HD], F32)
+                live["o_v", i // PAIR] = o_v
+            o_v = live["o_v", i // PAIR]
+            nc.scalar.copy(
+                out=o_v[:, :, jj, :], in_=live["u_kv", i][:, v_cols].rearrange("p (h d) -> p h d", h=V_HEADS)
+            )
             nc.scalar.activation(out=u_rstd[:], in_=u_sum[:], func=ACT.Abs_reciprocal_sqrt, scale=1.0 / HD, bias=EPS)
             live["u_rstd", i] = u_rstd
+            if jj == PAIR - 1:
+                b, j0 = pairs[i // PAIR]
+                nc.sync.dma_start(out=out_2[b].rearrange("h (p j) d -> p h j d", j=J)[:, :, j0 : j0 + PAIR, :], in_=o_v[:])
 
         def rope_and_store(i):
             b, j0 = pairs[i // PAIR]
@@ -316,15 +310,23 @@ def tile_rawkvinjector_pa_t_kernel(
             if index is not None:
                 one_stage(index)
 
-        table_steps = BATCH * TABLE_J
-        build_tables(0, nc.gpsimd)
+        parts = [(table, half) for table in range(2) for half in range(2)]
+        pairs_of_chunk = BATCH * TABLE_J // PAIR
+        assert len(parts) == pairs_of_chunk
+        for j0 in (0, TABLE_J):
+            for table, half in parts:
+                build_table_part(j0, table, half)
+
         for step in range(PAIR * len(pairs) + LAG_ROPE):
-            run(sum_x_squares, pair_at(step, 0))
             run(quantise, pair_at(step, LAG_QUANTISE))
-            if step % table_steps == LAG_QUANTISE and (step // table_steps + 1) * TABLE_J < J:
-                build_tables((step // table_steps + 1) * TABLE_J, nc.vector)
             run(multiply, tile_at(step, LAG_MATMUL))
-            run(normalise_and_transpose, pair_at(step, LAG_H))
-            run(regroup, pair_at(step, LAG_REGROUP))
-            run(copy_v_and_sum_squares, tile_at(step, LAG_SQUARES))
+            run(sum_squares_and_copy_v, tile_at(step, LAG_SQUARES))
             run(rope_and_store, tile_at(step, LAG_ROPE))
+            summed = pair_at(step, LAG_ROPE + PAIR - 1)
+            if summed is not None and (summed // pairs_of_chunk + 2) * TABLE_J < J:
+                table, half = parts[summed % pairs_of_chunk]
+                build_table_part((summed // pairs_of_chunk + 2) * TABLE_J, table, half)
+            run(sum_x_squares, pair_at(step, 0))
+            run(regroup, pair_at(step, LAG_REGROUP))
+            run(x_rsqrt, pair_at(step, 0))
+            run(normalise_and_transpose, pair_at(step, LAG_H))

@@ -33,10 +33,10 @@ FLOPS = 2 * BATCH * T * D * (Q_HEADS + K_HEADS + V_HEADS) * HD
 
 LAG_H = 1
 LAG_REGROUP = 2
-LAG_QUANTISE = 5
-LAG_MATMUL = 5
-LAG_SQUARES = 6
-LAG_ROPE = 7
+RUN_AHEAD = 2
+LAG_MATMUL = 3
+LAG_SQUARES = 4
+LAG_ROPE = 5
 
 
 def tile_rawkvinjector_pa_t_kernel(
@@ -68,24 +68,25 @@ def tile_rawkvinjector_pa_t_kernel(
         ctx.enter_context(tc.manual_schedule())
 
         x_sb = keep.tile([P, BATCH, J, D], BF16)
-        ln_w_sb = keep.tile([P, D], BF16)
+        rows = keep.tile([P, D + 2 * HD], BF16)
         norm_w = keep.tile([P, 2, HD], BF16)
         neg_w = keep.tile([P, 2, HALF], BF16)
         cos_sb = keep.tile([P, J, HD], BF16)
         sin_sb = keep.tile([P, J, HD], BF16)
         tables = keep.tile([P, 2, J, 2, HD], F32)
         ident = keep.tile([P, P], F32)
-        ident_bf = keep.tile([P, P], BF16)
+        ones = keep.tile([P, P], BF16)
         wq_words = keep.tile([P, Q_HEADS * HD], U32, align_bytes=64)
         wkv_words = keep.tile([P, (K_HEADS + V_HEADS) * HD], U32, align_bytes=64)
         wq_scales = keep.tile([P, Q_HEADS * HD], U8, align_bytes=64)
         wkv_scales = keep.tile([P, (K_HEADS + V_HEADS) * HD], U8, align_bytes=64)
         one = keep.tile([P, 1], F32)
 
+        nc.vector.memset(rows[:], 0.0)
+        nc.vector.memset(ones[:], 1.0)
         nc.vector.memset(wq_scales[:].bitcast(I32), 0)
         nc.vector.memset(wkv_scales[:].bitcast(I32), 0)
         nc.vector.memset(one[:], 1.0)
-        make_identity(nc, ident_bf[:])
         make_identity(nc, ident[:])
 
         x_dram = hidden_states.rearrange("b (p j) k -> p b j k", j=J)
@@ -107,9 +108,9 @@ def tile_rawkvinjector_pa_t_kernel(
 
         k_cols = slice(0, K_HEADS * HD)
         v_cols = slice(K_HEADS * HD, (K_HEADS + V_HEADS) * HD)
-        nc.scalar.dma_start(out=ln_w_sb[:], in_=ln1_w.partition_broadcast(P))
-        nc.scalar.dma_start(out=norm_w[:, 0, :], in_=q_norm_w.partition_broadcast(P))
-        nc.scalar.dma_start(out=norm_w[:, 1, :], in_=k_norm_w.partition_broadcast(P))
+        nc.scalar.dma_start(out=rows[0:1, 0:D], in_=ln1_w.rearrange("(o k) -> o k", o=1))
+        nc.scalar.dma_start(out=rows[0:1, D : D + HD], in_=q_norm_w.rearrange("(o k) -> o k", o=1))
+        nc.scalar.dma_start(out=rows[0:1, D + HD : D + 2 * HD], in_=k_norm_w.rearrange("(o k) -> o k", o=1))
         cos_dram = cos.rearrange("(p j) d -> p j d", j=J)
         sin_dram = sin.rearrange("(p j) d -> p j d", j=J)
 
@@ -118,6 +119,7 @@ def tile_rawkvinjector_pa_t_kernel(
             nc.sync.dma_start(out=sin_sb[:, j0:j1, :], in_=sin_dram[:, j0:j1, :])
 
         load_x(0, 0, PAIR)
+        load_x(1, 0, PAIR)
         load_cos_sin(0, TABLE_J)
         load_scales(wq_scales, slice(0, Q_HEADS * HD), Wq_scales)
         load_scales(wkv_scales, k_cols, Wk_scales)
@@ -125,7 +127,6 @@ def tile_rawkvinjector_pa_t_kernel(
         load_words(wq_words, slice(0, Q_HEADS * HD), Wq_words)
         load_words(wkv_words, k_cols, Wk_words)
         load_words(wkv_words, v_cols, Wv_words)
-        load_x(1, 0, PAIR)
         for b in range(BATCH):
             load_x(b, PAIR, X_LOAD)
         load_cos_sin(TABLE_J, J)
@@ -136,7 +137,10 @@ def tile_rawkvinjector_pa_t_kernel(
         nc.scalar.activation(out=one[:], in_=one[:], func=ACT.Abs_reciprocal_sqrt)
 
         ln_w = psum_w.tile([P, D], F32)
-        nc.tensor.matmul(out=ln_w[:], lhsT=ident_bf[:], rhs=ln_w_sb[:], start=True, stop=True)
+        nc.tensor.matmul(out=ln_w[:], lhsT=ones[:], rhs=rows[:, 0:D], start=True, stop=True)
+        norm_w_ps = psum_t.tile([P, 2 * HD], F32, name="h_t")
+        nc.tensor.matmul(out=norm_w_ps[:], lhsT=ones[:], rhs=rows[:, D : D + 2 * HD], start=True, stop=True)
+        nc.vector.tensor_copy(out=norm_w[:].rearrange("p a d -> p (a d)"), in_=norm_w_ps[:])
 
         nc.gpsimd.tensor_scalar(
             out=neg_w[:], in0=norm_w[:, :, HALF:HD], scalar1=-1.0, scalar2=0.0, op0=ALU.mult, op1=ALU.add
@@ -285,12 +289,20 @@ def tile_rawkvinjector_pa_t_kernel(
             o_qk = live["o_qk", i // PAIR]
             if (jj + 1) % together == 0:
                 jjs = slice(jj + 1 - together, jj + 1)
-                nc.gpsimd.tensor_tensor(
-                    out=o_qk[:, :, jjs, :].rearrange("p h j (x d) -> p j h x d", x=2),
-                    in0=products[:, jjs, :, 0, :].rearrange("p j h (x d) -> p j h x d", x=2),
-                    in1=products[:, jjs, :, 1, :].rearrange("p j h (x d) -> p j h x d", x=2)[:, :, :, ::-1, :],
-                    op=ALU.add,
-                )
+                if i == PAIR * len(pairs) - 1:
+                    nc.vector.tensor_tensor(
+                        out=o_qk[:, :, jj, :].rearrange("p h (x d) -> p h x d", x=2),
+                        in0=products[:, jj, :, 0, :].rearrange("p h (x d) -> p h x d", x=2),
+                        in1=products[:, jj, :, 1, :].rearrange("p h (x d) -> p h x d", x=2)[:, :, ::-1, :],
+                        op=ALU.add,
+                    )
+                else:
+                    nc.gpsimd.tensor_tensor(
+                        out=o_qk[:, :, jjs, :].rearrange("p h j (x d) -> p j h x d", x=2),
+                        in0=products[:, jjs, :, 0, :].rearrange("p j h (x d) -> p j h x d", x=2),
+                        in1=products[:, jjs, :, 1, :].rearrange("p j h (x d) -> p j h x d", x=2)[:, :, :, ::-1, :],
+                        op=ALU.add,
+                    )
                 js = slice(j0 + jj + 1 - together, j0 + jj + 1)
                 for dram, heads in ((out_0, slice(0, Q_HEADS)), (out_1, slice(Q_HEADS, ROPE_HEADS))):
                     nc.sync.dma_start(
@@ -302,6 +314,13 @@ def tile_rawkvinjector_pa_t_kernel(
             if first % PAIR == 0 and 0 <= first // PAIR < len(pairs):
                 return first // PAIR
             return None
+
+        def front_start(n):
+            return max(n, PAIR * n - RUN_AHEAD)
+
+        def front_at(step, lag):
+            found = [n for n in range(len(pairs)) if front_start(n) + lag == step]
+            return found[0] if found else None
 
         def tile_at(step, lag):
             return step - lag if 0 <= step - lag < PAIR * len(pairs) else None
@@ -318,7 +337,7 @@ def tile_rawkvinjector_pa_t_kernel(
                 build_table_part(j0, table, half)
 
         for step in range(PAIR * len(pairs) + LAG_ROPE):
-            run(quantise, pair_at(step, LAG_QUANTISE))
+            run(quantise, pair_at(step, LAG_MATMUL))
             run(multiply, tile_at(step, LAG_MATMUL))
             run(sum_squares_and_copy_v, tile_at(step, LAG_SQUARES))
             run(rope_and_store, tile_at(step, LAG_ROPE))
@@ -326,7 +345,7 @@ def tile_rawkvinjector_pa_t_kernel(
             if summed is not None and (summed // pairs_of_chunk + 2) * TABLE_J < J:
                 table, half = parts[summed % pairs_of_chunk]
                 build_table_part((summed // pairs_of_chunk + 2) * TABLE_J, table, half)
-            run(sum_x_squares, pair_at(step, 0))
-            run(regroup, pair_at(step, LAG_REGROUP))
-            run(x_rsqrt, pair_at(step, 0))
-            run(normalise_and_transpose, pair_at(step, LAG_H))
+            run(sum_x_squares, front_at(step, 0))
+            run(regroup, front_at(step, LAG_REGROUP))
+            run(x_rsqrt, front_at(step, 0))
+            run(normalise_and_transpose, front_at(step, LAG_H))

@@ -114,22 +114,23 @@ def tile_rawkvinjector_pa_t_kernel(
         cos_dram = cos.rearrange("(p j) d -> p j d", j=J)
         sin_dram = sin.rearrange("(p j) d -> p j d", j=J)
 
-        def load_cos_sin(j0, j1):
-            nc.sync.dma_start(out=cos_sb[:, j0:j1, :], in_=cos_dram[:, j0:j1, :])
-            nc.sync.dma_start(out=sin_sb[:, j0:j1, :], in_=sin_dram[:, j0:j1, :])
+        def load_cos_sin(queue, j0, j1):
+            queue.dma_start(out=cos_sb[:, j0:j1, :], in_=cos_dram[:, j0:j1, :])
+            queue.dma_start(out=sin_sb[:, j0:j1, :], in_=sin_dram[:, j0:j1, :])
 
         load_x(0, 0, PAIR)
         load_x(1, 0, PAIR)
-        load_cos_sin(0, TABLE_J)
+        load_cos_sin(nc.sync, 0, TABLE_J)
+        load_x(0, PAIR, X_LOAD)
+        load_cos_sin(nc.gpsimd, TABLE_J, 2 * TABLE_J)
+        load_cos_sin(nc.gpsimd, 2 * TABLE_J, J)
         load_scales(wq_scales, slice(0, Q_HEADS * HD), Wq_scales)
         load_scales(wkv_scales, k_cols, Wk_scales)
         load_scales(wkv_scales, v_cols, Wv_scales)
         load_words(wq_words, slice(0, Q_HEADS * HD), Wq_words)
         load_words(wkv_words, k_cols, Wk_words)
         load_words(wkv_words, v_cols, Wv_words)
-        for b in range(BATCH):
-            load_x(b, PAIR, X_LOAD)
-        load_cos_sin(TABLE_J, J)
+        load_x(1, PAIR, X_LOAD)
         for j0 in range(X_LOAD, J, X_LOAD):
             for b in range(BATCH):
                 load_x(b, j0, j0 + X_LOAD)
@@ -142,17 +143,17 @@ def tile_rawkvinjector_pa_t_kernel(
         nc.tensor.matmul(out=norm_w_ps[:], lhsT=ones[:], rhs=rows[:, D : D + 2 * HD], start=True, stop=True)
         nc.vector.tensor_copy(out=norm_w[:].rearrange("p a d -> p (a d)"), in_=norm_w_ps[:])
 
-        nc.gpsimd.tensor_scalar(
+        nc.vector.tensor_scalar(
             out=neg_w[:], in0=norm_w[:, :, HALF:HD], scalar1=-1.0, scalar2=0.0, op0=ALU.mult, op1=ALU.add
         )
 
-        def build_table_part(j0, table, half):
+        def build_table_part(engine, j0, table, half):
             js = slice(j0, j0 + TABLE_J)
             here = slice(half * HALF, (half + 1) * HALF)
             other = slice((1 - half) * HALF, (2 - half) * HALF)
             trig = cos_sb[:, js, here] if table == 0 else sin_sb[:, js, other]
             weight = neg_w[:] if (table, half) == (1, 1) else norm_w[:, :, here]
-            nc.gpsimd.tensor_tensor(
+            engine.tensor_tensor(
                 out=tables[:, :, js, table, here],
                 in0=trig.unsqueeze(1).to_broadcast([P, 2, TABLE_J, HALF]),
                 in1=weight.unsqueeze(2).to_broadcast([P, 2, TABLE_J, HALF]),
@@ -282,32 +283,45 @@ def tile_rawkvinjector_pa_t_kernel(
                     op0=ALU.mult,
                     op1=ALU.mult,
                 )
-            together = 1 if i // PAIR == len(pairs) - 1 else PAIR
             if jj == 0:
                 o_qk = stage.tile([P, ROPE_HEADS, PAIR, HD], F32)
                 live["o_qk", i // PAIR] = o_qk
             o_qk = live["o_qk", i // PAIR]
-            if (jj + 1) % together == 0:
-                jjs = slice(jj + 1 - together, jj + 1)
-                if i == PAIR * len(pairs) - 1:
-                    nc.vector.tensor_tensor(
-                        out=o_qk[:, :, jj, :].rearrange("p h (x d) -> p h x d", x=2),
-                        in0=products[:, jj, :, 0, :].rearrange("p h (x d) -> p h x d", x=2),
-                        in1=products[:, jj, :, 1, :].rearrange("p h (x d) -> p h x d", x=2)[:, :, ::-1, :],
-                        op=ALU.add,
-                    )
-                else:
+            q_heads, k_heads = slice(0, Q_HEADS), slice(Q_HEADS, ROPE_HEADS)
+
+            def add_tile(engine, heads, tile_jj):
+                engine.tensor_tensor(
+                    out=o_qk[:, heads, tile_jj, :].rearrange("p h (x d) -> p h x d", x=2),
+                    in0=products[:, tile_jj, heads, 0, :].rearrange("p h (x d) -> p h x d", x=2),
+                    in1=products[:, tile_jj, heads, 1, :].rearrange("p h (x d) -> p h x d", x=2)[:, :, ::-1, :],
+                    op=ALU.add,
+                )
+
+            def store(dram, heads, jjs):
+                nc.sync.dma_start(
+                    out=dram[b].rearrange("h (p j) d -> p h j d", j=J)[:, :, j0 + jjs.start : j0 + jjs.stop, :],
+                    in_=o_qk[:, heads, jjs, :],
+                )
+
+            if i // PAIR < len(pairs) - 1:
+                if jj == PAIR - 1:
                     nc.gpsimd.tensor_tensor(
-                        out=o_qk[:, :, jjs, :].rearrange("p h j (x d) -> p j h x d", x=2),
-                        in0=products[:, jjs, :, 0, :].rearrange("p j h (x d) -> p j h x d", x=2),
-                        in1=products[:, jjs, :, 1, :].rearrange("p j h (x d) -> p j h x d", x=2)[:, :, :, ::-1, :],
+                        out=o_qk[:].rearrange("p h j (x d) -> p j h x d", x=2),
+                        in0=products[:, :, :, 0, :].rearrange("p j h (x d) -> p j h x d", x=2),
+                        in1=products[:, :, :, 1, :].rearrange("p j h (x d) -> p j h x d", x=2)[:, :, :, ::-1, :],
                         op=ALU.add,
                     )
-                js = slice(j0 + jj + 1 - together, j0 + jj + 1)
-                for dram, heads in ((out_0, slice(0, Q_HEADS)), (out_1, slice(Q_HEADS, ROPE_HEADS))):
-                    nc.sync.dma_start(
-                        out=dram[b].rearrange("h (p j) d -> p h j d", j=J)[:, :, js, :], in_=o_qk[:, heads, jjs, :]
-                    )
+                    store(out_0, q_heads, slice(0, PAIR))
+                    store(out_1, k_heads, slice(0, PAIR))
+            elif jj == 0:
+                add_tile(nc.gpsimd, q_heads, 0)
+                store(out_0, q_heads, slice(0, 1))
+            else:
+                add_tile(nc.vector, q_heads, 1)
+                store(out_0, q_heads, slice(1, PAIR))
+                add_tile(nc.vector, k_heads, 0)
+                add_tile(nc.vector, k_heads, 1)
+                store(out_1, k_heads, slice(0, PAIR))
 
         def pair_at(step, lag):
             first = step - lag
@@ -329,12 +343,14 @@ def tile_rawkvinjector_pa_t_kernel(
             if index is not None:
                 one_stage(index)
 
-        parts = [(table, half) for table in range(2) for half in range(2)]
-        pairs_of_chunk = BATCH * TABLE_J // PAIR
-        assert len(parts) == pairs_of_chunk
-        for j0 in (0, TABLE_J):
-            for table, half in parts:
-                build_table_part(j0, table, half)
+        parts = [(j0, table, half) for j0 in range(0, J, TABLE_J) for table in range(2) for half in range(2)]
+        built = {"parts": 0}
+        vector_parts = {0: 2, 1: 1, 2: 1, 3: 4}
+
+        def build_next_part(engine):
+            j0, table, half = parts[built["parts"]]
+            built["parts"] = built["parts"] + 1
+            build_table_part(engine, j0, table, half)
 
         for step in range(PAIR * len(pairs) + LAG_ROPE):
             run(quantise, pair_at(step, LAG_MATMUL))
@@ -342,10 +358,11 @@ def tile_rawkvinjector_pa_t_kernel(
             run(sum_squares_and_copy_v, tile_at(step, LAG_SQUARES))
             run(rope_and_store, tile_at(step, LAG_ROPE))
             summed = pair_at(step, LAG_ROPE + PAIR - 1)
-            if summed is not None and (summed // pairs_of_chunk + 2) * TABLE_J < J:
-                table, half = parts[summed % pairs_of_chunk]
-                build_table_part((summed // pairs_of_chunk + 2) * TABLE_J, table, half)
-            run(sum_x_squares, front_at(step, 0))
+            if summed is not None and built["parts"] < len(parts):
+                build_next_part(nc.gpsimd)
             run(regroup, front_at(step, LAG_REGROUP))
+            run(sum_x_squares, front_at(step, 0))
             run(x_rsqrt, front_at(step, 0))
             run(normalise_and_transpose, front_at(step, LAG_H))
+            for count in range(vector_parts.get(step, 0)):
+                build_next_part(nc.vector)

@@ -125,9 +125,9 @@ def tile_rawkvinjector_pa_t_kernel(
         load_cos_sin(nc.gpsimd, TABLE_J, 2 * TABLE_J)
         load_cos_sin(nc.gpsimd, 2 * TABLE_J, J)
         load_scales(wq_scales, slice(0, Q_HEADS * HD), Wq_scales)
+        load_words(wq_words, slice(0, Q_HEADS * HD), Wq_words)
         load_scales(wkv_scales, k_cols, Wk_scales)
         load_scales(wkv_scales, v_cols, Wv_scales)
-        load_words(wq_words, slice(0, Q_HEADS * HD), Wq_words)
         load_words(wkv_words, k_cols, Wk_words)
         load_words(wkv_words, v_cols, Wv_words)
         load_x(1, PAIR, X_LOAD)
@@ -345,12 +345,16 @@ def tile_rawkvinjector_pa_t_kernel(
 
         parts = [(j0, table, half) for j0 in range(0, J, TABLE_J) for table in range(2) for half in range(2)]
         built = {"parts": 0}
-        vector_parts = {0: 2, 1: 1, 2: 1, 3: 4}
+        parts_of_chunk = 4
+        vector_parts = {LAG_MATMUL: parts_of_chunk}
 
         def build_next_part(engine):
             j0, table, half = parts[built["parts"]]
             built["parts"] = built["parts"] + 1
             build_table_part(engine, j0, table, half)
+
+        for count in range(parts_of_chunk):
+            build_next_part(nc.gpsimd)
 
         for step in range(PAIR * len(pairs) + LAG_ROPE):
             run(quantise, pair_at(step, LAG_MATMUL))

@@ -118,7 +118,8 @@ def tile_rawkvinjector_pa_t_kernel(
             queue.dma_start(out=cos_sb[:, j0:j1, :], in_=cos_dram[:, j0:j1, :])
             queue.dma_start(out=sin_sb[:, j0:j1, :], in_=sin_dram[:, j0:j1, :])
 
-        load_x(0, 0, PAIR)
+        load_x(0, 0, 1)
+        load_x(0, 1, PAIR)
         load_x(1, 0, PAIR)
         load_cos_sin(nc.sync, 0, TABLE_J)
         load_x(0, PAIR, X_LOAD)
@@ -167,6 +168,9 @@ def tile_rawkvinjector_pa_t_kernel(
             b, j0 = pairs[n]
             x_squares = stage.tile([P, PAIR, D], BF16)
             x_sum = small.tile([P, PAIR], F32)
+            x_rstd = small.tile([P, PAIR], F32)
+            live["x_sum", n] = x_sum
+            live["x_rstd", n] = x_rstd
             for jj in range(PAIR):
                 nc.scalar.activation(
                     out=x_squares[:, jj, :],
@@ -174,14 +178,21 @@ def tile_rawkvinjector_pa_t_kernel(
                     func=ACT.Square,
                     accum_out=x_sum[:, jj : jj + 1],
                 )
-            live["x_sum", n] = x_sum
+                if n == 0:
+                    x_rsqrt_columns(n, slice(jj, jj + 1))
+
+        def x_rsqrt_columns(n, jjs):
+            nc.scalar.activation(
+                out=live["x_rstd", n][:, jjs],
+                in_=live["x_sum", n][:, jjs],
+                func=ACT.Abs_reciprocal_sqrt,
+                scale=1.0 / D,
+                bias=EPS,
+            )
 
         def x_rsqrt(n):
-            x_rstd = small.tile([P, PAIR], F32)
-            nc.scalar.activation(
-                out=x_rstd[:], in_=live["x_sum", n][:], func=ACT.Abs_reciprocal_sqrt, scale=1.0 / D, bias=EPS
-            )
-            live["x_rstd", n] = x_rstd
+            if n > 0:
+                x_rsqrt_columns(n, slice(0, PAIR))
 
         def normalise_and_transpose(n):
             b, j0 = pairs[n]
@@ -314,9 +325,10 @@ def tile_rawkvinjector_pa_t_kernel(
                     store(out_0, q_heads, slice(0, PAIR))
                     store(out_1, k_heads, slice(0, PAIR))
             elif jj == 0:
-                add_tile(nc.gpsimd, q_heads, 0)
-                store(out_0, q_heads, slice(0, 1))
+                add_tile(nc.gpsimd, slice(0, Q_HEADS - 1), 0)
             else:
+                add_tile(nc.vector, slice(Q_HEADS - 1, Q_HEADS), 0)
+                store(out_0, q_heads, slice(0, 1))
                 add_tile(nc.vector, q_heads, 1)
                 store(out_0, q_heads, slice(1, PAIR))
                 add_tile(nc.vector, k_heads, 0)
@@ -346,7 +358,7 @@ def tile_rawkvinjector_pa_t_kernel(
         parts = [(j0, table, half) for j0 in range(0, J, TABLE_J) for table in range(2) for half in range(2)]
         built = {"parts": 0}
         parts_of_chunk = 4
-        vector_parts = {LAG_MATMUL: parts_of_chunk}
+        vector_parts = {LAG_MATMUL: parts_of_chunk // 2}
 
         def build_next_part(engine):
             j0, table, half = parts[built["parts"]]

@@ -281,13 +281,13 @@ def tile_rawkvinjector_pa_t_kernel(
             jj = i % PAIR
             u_rstd = live["u_rstd", i]
             if jj == 0:
-                products = stage.tile([P, PAIR, ROPE_HEADS, 2, HD], F32)
+                products = stage.tile([P, 2, ROPE_HEADS, PAIR, HD], F32)
                 live["products", i // PAIR] = products
             products = live["products", i // PAIR]
             for head in range(ROPE_HEADS):
                 q_or_k = 0 if head < Q_HEADS else 1
                 nc.vector.scalar_tensor_tensor(
-                    out=products[:, jj, head, :, :],
+                    out=products[:, :, head, jj, :],
                     in0=head_of(i, head).unsqueeze(1).to_broadcast([P, 2, HD]),
                     scalar=u_rstd[:, head : head + 1],
                     in1=tables[:, q_or_k, j0 + jj, :, :],
@@ -303,8 +303,8 @@ def tile_rawkvinjector_pa_t_kernel(
             def add_tile(engine, heads, tile_jj):
                 engine.tensor_tensor(
                     out=o_qk[:, heads, tile_jj, :].rearrange("p h (x d) -> p h x d", x=2),
-                    in0=products[:, tile_jj, heads, 0, :].rearrange("p h (x d) -> p h x d", x=2),
-                    in1=products[:, tile_jj, heads, 1, :].rearrange("p h (x d) -> p h x d", x=2)[:, :, ::-1, :],
+                    in0=products[:, 0, heads, tile_jj, :].rearrange("p h (x d) -> p h x d", x=2),
+                    in1=products[:, 1, heads, tile_jj, :].rearrange("p h (x d) -> p h x d", x=2)[:, :, ::-1, :],
                     op=ALU.add,
                 )
 
@@ -317,9 +317,9 @@ def tile_rawkvinjector_pa_t_kernel(
             if i // PAIR < len(pairs) - 1:
                 if jj == PAIR - 1:
                     nc.gpsimd.tensor_tensor(
-                        out=o_qk[:].rearrange("p h j (x d) -> p j h x d", x=2),
-                        in0=products[:, :, :, 0, :].rearrange("p j h (x d) -> p j h x d", x=2),
-                        in1=products[:, :, :, 1, :].rearrange("p j h (x d) -> p j h x d", x=2)[:, :, :, ::-1, :],
+                        out=o_qk[:].rearrange("p h j (x d) -> p (h j) x d", x=2),
+                        in0=products[:, 0, :, :, :].rearrange("p h j (x d) -> p (h j) x d", x=2),
+                        in1=products[:, 1, :, :, :].rearrange("p h j (x d) -> p (h j) x d", x=2)[:, :, ::-1, :],
                         op=ALU.add,
                     )
                     store(out_0, q_heads, slice(0, PAIR))

@@ -376,8 +376,11 @@ def tile_rawkvinjector_pa_t_kernel(
             summed = pair_at(step, LAG_ROPE + PAIR - 1)
             if summed is not None and built["parts"] < len(parts):
                 build_next_part(nc.gpsimd)
-            run(regroup, front_at(step, LAG_REGROUP))
+            if tile_at(step, LAG_SQUARES) is None:
+                run(regroup, front_at(step, LAG_REGROUP))
             run(sum_x_squares, front_at(step, 0))
+            if tile_at(step, LAG_SQUARES) is not None:
+                run(regroup, front_at(step, LAG_REGROUP))
             run(x_rsqrt, front_at(step, 0))
             run(normalise_and_transpose, front_at(step, LAG_H))
             for count in range(vector_parts.get(step, 0)):

@@ -69,8 +69,8 @@ def tile_rawkvinjector_pa_t_kernel(
 
         x_sb = keep.tile([P, BATCH, J, D], BF16)
         rows = keep.tile([P, D + 2 * HD], BF16)
-        norm_w = keep.tile([P, 2, HD], BF16)
-        neg_w = keep.tile([P, 2, HALF], BF16)
+        norm_w = {"vector": keep.tile([P, 2, HD], BF16, name="norm_w_v"), "gpsimd": keep.tile([P, 2, HD], BF16, name="norm_w_g")}
+        neg_w = {"vector": keep.tile([P, 2, HALF], BF16, name="neg_w_v"), "gpsimd": keep.tile([P, 2, HALF], BF16, name="neg_w_g")}
         cos_sb = keep.tile([P, J, HD], BF16)
         sin_sb = keep.tile([P, J, HD], BF16)
         tables = keep.tile([P, 2, J, 2, HD], F32)
@@ -82,17 +82,16 @@ def tile_rawkvinjector_pa_t_kernel(
         wkv_scales = keep.tile([P, (K_HEADS + V_HEADS) * HD], U8, align_bytes=64)
         one = keep.tile([P, 1], F32)
 
+        nc.vector.memset(one[:], 1.0)
         nc.vector.memset(rows[:], 0.0)
         nc.vector.memset(ones[:], 1.0)
         nc.vector.memset(wq_scales[:].bitcast(I32), 0)
         nc.vector.memset(wkv_scales[:].bitcast(I32), 0)
-        nc.vector.memset(one[:], 1.0)
-        make_identity(nc, ident[:])
 
         x_dram = hidden_states.rearrange("b (p j) k -> p b j k", j=J)
 
-        def load_x(b, j0, j1):
-            nc.sync.dma_start(out=x_sb[:, b, j0:j1, :], in_=x_dram[:, b, j0:j1, :])
+        def load_x(b, j0, j1, queue=nc.sync):
+            queue.dma_start(out=x_sb[:, b, j0:j1, :], in_=x_dram[:, b, j0:j1, :])
 
         def load_scales(plane, cols, scales):
             for quadrant in range(P // 32):
@@ -108,9 +107,6 @@ def tile_rawkvinjector_pa_t_kernel(
 
         k_cols = slice(0, K_HEADS * HD)
         v_cols = slice(K_HEADS * HD, (K_HEADS + V_HEADS) * HD)
-        nc.scalar.dma_start(out=rows[0:1, 0:D], in_=ln1_w.rearrange("(o k) -> o k", o=1))
-        nc.scalar.dma_start(out=rows[0:1, D : D + HD], in_=q_norm_w.rearrange("(o k) -> o k", o=1))
-        nc.scalar.dma_start(out=rows[0:1, D + HD : D + 2 * HD], in_=k_norm_w.rearrange("(o k) -> o k", o=1))
         cos_dram = cos.rearrange("(p j) d -> p j d", j=J)
         sin_dram = sin.rearrange("(p j) d -> p j d", j=J)
 
@@ -118,13 +114,15 @@ def tile_rawkvinjector_pa_t_kernel(
             queue.dma_start(out=cos_sb[:, j0:j1, :], in_=cos_dram[:, j0:j1, :])
             queue.dma_start(out=sin_sb[:, j0:j1, :], in_=sin_dram[:, j0:j1, :])
 
+        load_x(1, 0, PAIR, nc.gpsimd)
+        make_identity(nc, ident[:])
+        load_x(0, PAIR, X_LOAD, nc.gpsimd)
+        load_cos_sin(nc.gpsimd, 0, TABLE_J)
         load_x(0, 0, 1)
         load_x(0, 1, PAIR)
-        load_x(1, 0, PAIR)
-        load_cos_sin(nc.sync, 0, TABLE_J)
-        load_x(0, PAIR, X_LOAD)
-        load_cos_sin(nc.gpsimd, TABLE_J, 2 * TABLE_J)
-        load_cos_sin(nc.gpsimd, 2 * TABLE_J, J)
+        nc.sync.dma_start(out=rows[0:1, 0:D], in_=ln1_w.rearrange("(o k) -> o k", o=1))
+        nc.sync.dma_start(out=rows[0:1, D : D + HD], in_=q_norm_w.rearrange("(o k) -> o k", o=1))
+        nc.sync.dma_start(out=rows[0:1, D + HD : D + 2 * HD], in_=k_norm_w.rearrange("(o k) -> o k", o=1))
         load_scales(wq_scales, slice(0, Q_HEADS * HD), Wq_scales)
         load_words(wq_words, slice(0, Q_HEADS * HD), Wq_words)
         load_scales(wkv_scales, k_cols, Wk_scales)
@@ -132,6 +130,8 @@ def tile_rawkvinjector_pa_t_kernel(
         load_words(wkv_words, k_cols, Wk_words)
         load_words(wkv_words, v_cols, Wv_words)
         load_x(1, PAIR, X_LOAD)
+        load_cos_sin(nc.sync, TABLE_J, 2 * TABLE_J)
+        load_cos_sin(nc.sync, 2 * TABLE_J, J)
         for j0 in range(X_LOAD, J, X_LOAD):
             for b in range(BATCH):
                 load_x(b, j0, j0 + X_LOAD)
@@ -140,46 +140,66 @@ def tile_rawkvinjector_pa_t_kernel(
 
         ln_w = psum_w.tile([P, D], F32)
         nc.tensor.matmul(out=ln_w[:], lhsT=ones[:], rhs=rows[:, 0:D], start=True, stop=True)
-        norm_w_ps = psum_t.tile([P, 2 * HD], F32, name="h_t")
+        norm_w_ps = psum_u.tile([P, 2 * HD], F32, name="u_q")
         nc.tensor.matmul(out=norm_w_ps[:], lhsT=ones[:], rhs=rows[:, D : D + 2 * HD], start=True, stop=True)
-        nc.vector.tensor_copy(out=norm_w[:].rearrange("p a d -> p (a d)"), in_=norm_w_ps[:])
 
-        nc.vector.tensor_scalar(
-            out=neg_w[:], in0=norm_w[:, :, HALF:HD], scalar1=-1.0, scalar2=0.0, op0=ALU.mult, op1=ALU.add
-        )
+        def move_norm_weights(user):
+            if user == "vector":
+                nc.vector.tensor_copy(out=norm_w[user][:].rearrange("p a d -> p (a d)"), in_=norm_w_ps[:])
+            else:
+                nc.vector.tensor_copy(out=norm_w[user][:], in_=norm_w["vector"][:])
+            nc.vector.tensor_scalar(
+                out=neg_w[user][:], in0=norm_w["vector"][:, :, HALF:HD], scalar1=-1.0, scalar2=0.0, op0=ALU.mult, op1=ALU.add
+            )
 
-        def build_table_part(engine, j0, table, half):
-            js = slice(j0, j0 + TABLE_J)
+        def build_table_part(user, j0, j1, table, half):
+            js = slice(j0, j1)
             here = slice(half * HALF, (half + 1) * HALF)
             other = slice((1 - half) * HALF, (2 - half) * HALF)
             trig = cos_sb[:, js, here] if table == 0 else sin_sb[:, js, other]
-            weight = neg_w[:] if (table, half) == (1, 1) else norm_w[:, :, here]
+            weight = neg_w[user][:] if (table, half) == (1, 1) else norm_w[user][:, :, here]
+            engine = nc.vector if user == "vector" else nc.gpsimd
             engine.tensor_tensor(
                 out=tables[:, :, js, table, here],
-                in0=trig.unsqueeze(1).to_broadcast([P, 2, TABLE_J, HALF]),
-                in1=weight.unsqueeze(2).to_broadcast([P, 2, TABLE_J, HALF]),
+                in0=trig.unsqueeze(1).to_broadcast([P, 2, j1 - j0, HALF]),
+                in1=weight.unsqueeze(2).to_broadcast([P, 2, j1 - j0, HALF]),
                 op=ALU.mult,
             )
 
         pairs = [(b, j0) for j0 in range(0, J, PAIR) for b in range(BATCH)]
         live = {}
 
-        def sum_x_squares(n):
+        def sum_x_squares_of_tile(n, jj):
             b, j0 = pairs[n]
-            x_squares = stage.tile([P, PAIR, D], BF16)
+            if jj == 0:
+                x_squares = stage.tile([P, PAIR, D], BF16)
+                x_sum = small.tile([P, PAIR], F32)
+                x_rstd = small.tile([P, PAIR], F32)
+                live["x_squares", n] = x_squares
+                live["x_sum", n] = x_sum
+                live["x_rstd", n] = x_rstd
+            nc.scalar.activation(
+                out=live["x_squares", n][:, jj, :],
+                in_=x_sb[:, b, j0 + jj, :],
+                func=ACT.Square,
+                accum_out=live["x_sum", n][:, jj : jj + 1],
+            )
+
+        def sum_x_squares(n):
+            for jj in range(PAIR):
+                sum_x_squares_of_tile(n, jj)
+
+        def sum_x_squares_on_vector(n):
+            b, j0 = pairs[n]
+            x_squares_v = keep.tile([P, PAIR, D], F32)
             x_sum = small.tile([P, PAIR], F32)
             x_rstd = small.tile([P, PAIR], F32)
             live["x_sum", n] = x_sum
             live["x_rstd", n] = x_rstd
             for jj in range(PAIR):
-                nc.scalar.activation(
-                    out=x_squares[:, jj, :],
-                    in_=x_sb[:, b, j0 + jj, :],
-                    func=ACT.Square,
-                    accum_out=x_sum[:, jj : jj + 1],
-                )
-                if n == 0:
-                    x_rsqrt_columns(n, slice(jj, jj + 1))
+                nc.vector.scalar_tensor_tensor(
+                    out=x_squares_v[:, jj, :], in0=x_sb[:, b, j0 + jj, :], scalar=1.0, in1=x_sb[:, b, j0 + jj, :],
+                    op0=ALU.mult, op1=ALU.mult, accum_out=x_sum[:, jj : jj + 1])
 
         def x_rsqrt_columns(n, jjs):
             nc.scalar.activation(
@@ -191,43 +211,68 @@ def tile_rawkvinjector_pa_t_kernel(
             )
 
         def x_rsqrt(n):
-            if n > 0:
-                x_rsqrt_columns(n, slice(0, PAIR))
+            x_rsqrt_columns(n, slice(0, PAIR))
+
+        def normalise_tile(n, jj):
+            b, j0 = pairs[n]
+            if jj == 0:
+                h = stage.tile([P, PAIR, D], BF16)
+                live["h", n] = h
+            nc.vector.scalar_tensor_tensor(
+                out=live["h", n][:, jj, :],
+                in0=x_sb[:, b, j0 + jj, :],
+                scalar=live["x_rstd", n][:, jj : jj + 1],
+                in1=ln_w[:],
+                op0=ALU.mult,
+                op1=ALU.mult,
+            )
+
+        def transpose_tile(n, jj, plane_out):
+            h_words = live["h", n][:, jj, :].bitcast(F32)
+            for u in range(2):
+                nc.tensor.transpose(plane_out(u), h_words[:, u : D // 2 : 2], ident[:])
 
         def normalise_and_transpose(n):
-            b, j0 = pairs[n]
-            x_rstd = live["x_rstd", n]
-            h = stage.tile([P, PAIR, D], BF16)
             for jj in range(PAIR):
-                nc.vector.scalar_tensor_tensor(
-                    out=h[:, jj, :],
-                    in0=x_sb[:, b, j0 + jj, :],
-                    scalar=x_rstd[:, jj : jj + 1],
-                    in1=ln_w[:],
-                    op0=ALU.mult,
-                    op1=ALU.mult,
-                )
+                normalise_tile(n, jj)
+            transpose_pair(n)
+
+        def transpose_pair(n):
             h_t = psum_t.tile([P, 2, PAIR * P], F32)
             for jj in range(PAIR):
-                h_words = h[:, jj, :].bitcast(F32)
-                for u in range(2):
-                    nc.tensor.transpose(h_t[:, u, jj * P : (jj + 1) * P], h_words[:, u : D // 2 : 2], ident[:])
+                transpose_tile(n, jj, lambda u: h_t[:, u, jj * P : (jj + 1) * P])
             live["h_t", n] = h_t
 
-        def regroup(n):
+        def new_grouped(n):
             grouped = stage.tile([P, PAIR * P * 4], BF16, align_bytes=64)
-            nc.scalar.copy(
-                out=grouped[:].bitcast(F32).rearrange("p (r u) -> p r u", u=2),
-                in_=live["h_t", n][:].rearrange("p u r -> p r u"),
-            )
             live["grouped", n] = grouped
 
-        def quantise(n):
+        def regroup_words(n, tokens, planes):
+            nc.scalar.copy(
+                out=live["grouped", n][:].bitcast(F32).rearrange("p (r u) -> p r u", u=2)[:, tokens, :],
+                in_=planes.rearrange("p u r -> p r u"),
+            )
+
+        def regroup(n):
+            new_grouped(n)
+            regroup_words(n, slice(0, PAIR * P), live["h_t", n][:])
+
+        def new_codes(n):
             h_codes = stage.tile([P, PAIR * P], U32, align_bytes=64)
             h_scales = stage.tile([P, PAIR * P], U8, align_bytes=64)
-            nc.vector.quantize_mx(out=h_codes[:].bitcast(FP8X4), scales=h_scales[:], in_=live["grouped", n][:])
             live["h_codes", n] = h_codes
             live["h_scales", n] = h_scales
+
+        def quantise_tokens(n, t0, t1):
+            nc.vector.quantize_mx(
+                out=live["h_codes", n][:, t0:t1].bitcast(FP8X4),
+                scales=live["h_scales", n][:, t0:t1],
+                in_=live["grouped", n][:, 4 * t0 : 4 * t1],
+            )
+
+        def quantise(n):
+            new_codes(n)
+            quantise_tokens(n, 0, PAIR * P)
 
         def multiply(i):
             tokens = slice((i % PAIR) * P, (i % PAIR + 1) * P)
@@ -274,7 +319,8 @@ def tile_rawkvinjector_pa_t_kernel(
             live["u_rstd", i] = u_rstd
             if jj == PAIR - 1:
                 b, j0 = pairs[i // PAIR]
-                nc.sync.dma_start(out=out_2[b].rearrange("h (p j) d -> p h j d", j=J)[:, :, j0 : j0 + PAIR, :], in_=o_v[:])
+                queue = nc.scalar if i // PAIR == len(pairs) - 1 else nc.sync
+                queue.dma_start(out=out_2[b].rearrange("h (p j) d -> p h j d", j=J)[:, :, j0 : j0 + PAIR, :], in_=o_v[:])
 
         def rope_and_store(i):
             b, j0 = pairs[i // PAIR]
@@ -314,7 +360,11 @@ def tile_rawkvinjector_pa_t_kernel(
                     in_=o_qk[:, heads, jjs, :],
                 )
 
-            if i // PAIR < len(pairs) - 1:
+            if i // PAIR == len(pairs) - 2:
+                add_tile(nc.gpsimd, slice(0, ROPE_HEADS), jj)
+                store(out_0, q_heads, slice(jj, jj + 1))
+                store(out_1, k_heads, slice(jj, jj + 1))
+            elif i // PAIR < len(pairs) - 1:
                 if jj == PAIR - 1:
                     nc.gpsimd.tensor_tensor(
                         out=o_qk[:].rearrange("p h j (x d) -> p (h j) x d", x=2),
@@ -324,16 +374,15 @@ def tile_rawkvinjector_pa_t_kernel(
                     )
                     store(out_0, q_heads, slice(0, PAIR))
                     store(out_1, k_heads, slice(0, PAIR))
-            elif jj == 0:
-                add_tile(nc.gpsimd, slice(0, Q_HEADS - 1), 0)
-            else:
-                add_tile(nc.vector, slice(Q_HEADS - 1, Q_HEADS), 0)
+            elif jj == PAIR - 1:
+                add_tile(nc.vector, q_heads, 0)
                 store(out_0, q_heads, slice(0, 1))
                 add_tile(nc.vector, q_heads, 1)
                 store(out_0, q_heads, slice(1, PAIR))
                 add_tile(nc.vector, k_heads, 0)
+                store(out_1, k_heads, slice(0, 1))
                 add_tile(nc.vector, k_heads, 1)
-                store(out_1, k_heads, slice(0, PAIR))
+                store(out_1, k_heads, slice(1, PAIR))
 
         def pair_at(step, lag):
             first = step - lag
@@ -351,22 +400,71 @@ def tile_rawkvinjector_pa_t_kernel(
         def tile_at(step, lag):
             return step - lag if 0 <= step - lag < PAIR * len(pairs) else None
 
+        done = set()
+
+        def start(one_stage, index):
+            one_stage(index)
+            done.add((one_stage, index))
+
         def run(one_stage, index):
-            if index is not None:
+            if index is not None and (one_stage, index) not in done:
                 one_stage(index)
 
-        parts = [(j0, table, half) for j0 in range(0, J, TABLE_J) for table in range(2) for half in range(2)]
+        chunks = [(0, PAIR), (PAIR, TABLE_J)] + [(j0, j0 + TABLE_J) for j0 in range(TABLE_J, J, TABLE_J)]
+        parts = [(j0, j1, table, half) for j0, j1 in chunks for table in range(2) for half in range(2)]
         built = {"parts": 0}
-        parts_of_chunk = 4
-        vector_parts = {LAG_MATMUL: parts_of_chunk // 2}
 
-        def build_next_part(engine):
-            j0, table, half = parts[built["parts"]]
-            built["parts"] = built["parts"] + 1
-            build_table_part(engine, j0, table, half)
+        def build_parts(user, count):
+            for part in range(count):
+                j0, j1, table, half = parts[built["parts"]]
+                built["parts"] = built["parts"] + 1
+                build_table_part(user, j0, j1, table, half)
 
-        for count in range(parts_of_chunk):
-            build_next_part(nc.gpsimd)
+        for jj in range(PAIR):
+            sum_x_squares_of_tile(0, jj)
+            x_rsqrt_columns(0, slice(jj, jj + 1))
+        done.add((sum_x_squares, 0))
+        done.add((x_rsqrt, 0))
+        normalise_tile(0, 0)
+        first_t = psum_u.tile([P, 2, P], F32, name="u_q")
+        transpose_tile(0, 0, lambda u: first_t[:, u, :])
+        start(sum_x_squares, 1)
+        start(x_rsqrt, 1)
+        normalise_tile(0, 1)
+        move_norm_weights("vector")
+        second_t = psum_t.tile([P, 2, P], F32, name="h_t")
+        transpose_tile(0, 1, lambda u: second_t[:, u, :])
+        done.add((normalise_and_transpose, 0))
+        new_grouped(0)
+        new_codes(0)
+        regroup_words(0, slice(0, P), first_t[:])
+        normalise_tile(1, 0)
+        quantise_tokens(0, 0, P)
+        start(multiply, 0)
+        sum_x_squares_of_tile(2, 0)
+        normalise_tile(1, 1)
+        regroup_words(0, slice(P, PAIR * P), second_t[:])
+        done.add((regroup, 0))
+        transpose_pair(1)
+        done.add((normalise_and_transpose, 1))
+        sum_x_squares_of_tile(2, 1)
+        done.add((sum_x_squares, 2))
+        start(x_rsqrt, 2)
+        quantise_tokens(0, P, PAIR * P)
+        done.add((quantise, 0))
+        build_parts("vector", 2)
+        start(multiply, 1)
+        start(sum_squares_and_copy_v, 0)
+        start(regroup, 1)
+        start(normalise_and_transpose, 2)
+        build_parts("vector", 2)
+        sum_x_squares_on_vector(3)
+        done.add((sum_x_squares, 3))
+        start(sum_squares_and_copy_v, 1)
+        start(x_rsqrt, 3)
+        start(quantise, 1)
+        move_norm_weights("gpsimd")
+        build_parts("gpsimd", 5)
 
         for step in range(PAIR * len(pairs) + LAG_ROPE):
             run(quantise, pair_at(step, LAG_MATMUL))
@@ -375,13 +473,8 @@ def tile_rawkvinjector_pa_t_kernel(
             run(rope_and_store, tile_at(step, LAG_ROPE))
             summed = pair_at(step, LAG_ROPE + PAIR - 1)
             if summed is not None and built["parts"] < len(parts):
-                build_next_part(nc.gpsimd)
-            if tile_at(step, LAG_SQUARES) is None:
-                run(regroup, front_at(step, LAG_REGROUP))
+                build_parts("gpsimd", 1)
             run(sum_x_squares, front_at(step, 0))
-            if tile_at(step, LAG_SQUARES) is not None:
-                run(regroup, front_at(step, LAG_REGROUP))
+            run(regroup, front_at(step, LAG_REGROUP))
             run(x_rsqrt, front_at(step, 0))
             run(normalise_and_transpose, front_at(step, LAG_H))
-            for count in range(vector_parts.get(step, 0)):
-                build_next_part(nc.vector)

@@ -189,18 +189,6 @@ def tile_rawkvinjector_pa_t_kernel(
             for jj in range(PAIR):
                 sum_x_squares_of_tile(n, jj)
 
-        def sum_x_squares_on_vector(n):
-            b, j0 = pairs[n]
-            x_squares_v = keep.tile([P, PAIR, D], F32)
-            x_sum = small.tile([P, PAIR], F32)
-            x_rstd = small.tile([P, PAIR], F32)
-            live["x_sum", n] = x_sum
-            live["x_rstd", n] = x_rstd
-            for jj in range(PAIR):
-                nc.vector.scalar_tensor_tensor(
-                    out=x_squares_v[:, jj, :], in0=x_sb[:, b, j0 + jj, :], scalar=1.0, in1=x_sb[:, b, j0 + jj, :],
-                    op0=ALU.mult, op1=ALU.mult, accum_out=x_sum[:, jj : jj + 1])
-
         def x_rsqrt_columns(n, jjs):
             nc.scalar.activation(
                 out=live["x_rstd", n][:, jjs],
@@ -296,18 +284,23 @@ def tile_rawkvinjector_pa_t_kernel(
                 return live["u_q", i][:, head * HD : (head + 1) * HD]
             return live["u_kv", i][:, (head - Q_HEADS) * HD : (head - Q_HEADS + 1) * HD]
 
-        def sum_squares_and_copy_v(i):
-            jj = i % PAIR
-            u_squares = stage.tile([P, ROPE_HEADS, HD], BF16)
-            u_sum = small.tile([P, ROPE_HEADS], F32)
-            u_rstd = small.tile([P, ROPE_HEADS], F32)
-            for head in range(ROPE_HEADS):
+        def sum_squares(i, heads):
+            if heads.start == 0:
+                u_squares = stage.tile([P, ROPE_HEADS, HD], BF16)
+                u_sum = small.tile([P, ROPE_HEADS], F32)
+                live["u_squares", i] = u_squares
+                live["u_sum", i] = u_sum
+            for head in range(heads.start, heads.stop):
                 nc.scalar.activation(
-                    out=u_squares[:, head, :],
+                    out=live["u_squares", i][:, head, :],
                     in_=head_of(i, head),
                     func=ACT.Square,
-                    accum_out=u_sum[:, head : head + 1],
+                    accum_out=live["u_sum", i][:, head : head + 1],
                 )
+
+        def sum_k_squares_and_copy_v(i):
+            jj = i % PAIR
+            sum_squares(i, slice(Q_HEADS, ROPE_HEADS))
             if jj == 0:
                 o_v = stage.tile([P, V_HEADS, PAIR, HD], F32)
                 live["o_v", i // PAIR] = o_v
@@ -315,12 +308,17 @@ def tile_rawkvinjector_pa_t_kernel(
             nc.scalar.copy(
                 out=o_v[:, :, jj, :], in_=live["u_kv", i][:, v_cols].rearrange("p (h d) -> p h d", h=V_HEADS)
             )
-            nc.scalar.activation(out=u_rstd[:], in_=u_sum[:], func=ACT.Abs_reciprocal_sqrt, scale=1.0 / HD, bias=EPS)
+            u_rstd = small.tile([P, ROPE_HEADS], F32)
+            nc.scalar.activation(out=u_rstd[:], in_=live["u_sum", i][:], func=ACT.Abs_reciprocal_sqrt, scale=1.0 / HD, bias=EPS)
             live["u_rstd", i] = u_rstd
             if jj == PAIR - 1:
                 b, j0 = pairs[i // PAIR]
                 queue = nc.scalar if i // PAIR == len(pairs) - 1 else nc.sync
                 queue.dma_start(out=out_2[b].rearrange("h (p j) d -> p h j d", j=J)[:, :, j0 : j0 + PAIR, :], in_=o_v[:])
+
+        def sum_squares_and_copy_v(i):
+            sum_squares(i, slice(0, Q_HEADS))
+            sum_k_squares_and_copy_v(i)
 
         def rope_and_store(i):
             b, j0 = pairs[i // PAIR]
@@ -423,58 +421,59 @@ def tile_rawkvinjector_pa_t_kernel(
         for jj in range(PAIR):
             sum_x_squares_of_tile(0, jj)
             x_rsqrt_columns(0, slice(jj, jj + 1))
-        done.add((sum_x_squares, 0))
-        done.add((x_rsqrt, 0))
         normalise_tile(0, 0)
         first_t = psum_u.tile([P, 2, P], F32, name="u_q")
         transpose_tile(0, 0, lambda u: first_t[:, u, :])
-        start(sum_x_squares, 1)
-        start(x_rsqrt, 1)
+        sum_x_squares(1)
+        x_rsqrt(1)
         normalise_tile(0, 1)
         move_norm_weights("vector")
         second_t = psum_t.tile([P, 2, P], F32, name="h_t")
         transpose_tile(0, 1, lambda u: second_t[:, u, :])
-        done.add((normalise_and_transpose, 0))
         new_grouped(0)
         new_codes(0)
         regroup_words(0, slice(0, P), first_t[:])
         normalise_tile(1, 0)
         quantise_tokens(0, 0, P)
-        start(multiply, 0)
         sum_x_squares_of_tile(2, 0)
         normalise_tile(1, 1)
         regroup_words(0, slice(P, PAIR * P), second_t[:])
-        done.add((regroup, 0))
         transpose_pair(1)
-        done.add((normalise_and_transpose, 1))
         sum_x_squares_of_tile(2, 1)
-        done.add((sum_x_squares, 2))
-        start(x_rsqrt, 2)
+        x_rsqrt(2)
         quantise_tokens(0, P, PAIR * P)
-        done.add((quantise, 0))
+        multiply(0)
         build_parts("vector", 2)
-        start(multiply, 1)
-        start(sum_squares_and_copy_v, 0)
-        start(regroup, 1)
-        start(normalise_and_transpose, 2)
+        regroup(1)
+        sum_squares(0, slice(0, Q_HEADS))
+        normalise_tile(2, 0)
+        normalise_tile(2, 1)
         build_parts("vector", 2)
-        sum_x_squares_on_vector(3)
-        done.add((sum_x_squares, 3))
-        start(sum_squares_and_copy_v, 1)
-        start(x_rsqrt, 3)
-        start(quantise, 1)
+        sum_k_squares_and_copy_v(0)
+        multiply(1)
+        transpose_pair(2)
+        sum_squares_and_copy_v(1)
+        regroup(2)
+        quantise(1)
         move_norm_weights("gpsimd")
         build_parts("gpsimd", 5)
 
-        for step in range(PAIR * len(pairs) + LAG_ROPE):
-            run(quantise, pair_at(step, LAG_MATMUL))
-            run(multiply, tile_at(step, LAG_MATMUL))
-            run(sum_squares_and_copy_v, tile_at(step, LAG_SQUARES))
+        def pair_with(first, step):
+            n = (step - first) // PAIR
+            return n if (step - first) % PAIR == 0 and 3 <= n < len(pairs) else None
+
+        for step in range(4, PAIR * len(pairs) + LAG_ROPE):
+            if step > LAG_MATMUL + PAIR:
+                run(quantise, pair_at(step, LAG_MATMUL))
+            if step > LAG_MATMUL + 1:
+                run(multiply, tile_at(step, LAG_MATMUL))
+            run(normalise_and_transpose, pair_with(1, step))
+            if step > LAG_SQUARES + 1:
+                run(sum_squares_and_copy_v, tile_at(step, LAG_SQUARES))
             run(rope_and_store, tile_at(step, LAG_ROPE))
             summed = pair_at(step, LAG_ROPE + PAIR - 1)
             if summed is not None and built["parts"] < len(parts):
                 build_parts("gpsimd", 1)
-            run(sum_x_squares, front_at(step, 0))
-            run(regroup, front_at(step, LAG_REGROUP))
-            run(x_rsqrt, front_at(step, 0))
-            run(normalise_and_transpose, front_at(step, LAG_H))
+            run(sum_x_squares, pair_with(-1, step))
+            run(x_rsqrt, pair_with(-1, step))
+            run(regroup, pair_with(1, step))

@@ -114,17 +114,17 @@ def tile_rawkvinjector_pa_t_kernel(
             queue.dma_start(out=cos_sb[:, j0:j1, :], in_=cos_dram[:, j0:j1, :])
             queue.dma_start(out=sin_sb[:, j0:j1, :], in_=sin_dram[:, j0:j1, :])
 
-        load_x(1, 0, PAIR, nc.gpsimd)
         make_identity(nc, ident[:])
-        load_x(0, PAIR, X_LOAD, nc.gpsimd)
-        load_cos_sin(nc.gpsimd, 0, TABLE_J)
         load_x(0, 0, 1)
         load_x(0, 1, PAIR)
         nc.sync.dma_start(out=rows[0:1, 0:D], in_=ln1_w.rearrange("(o k) -> o k", o=1))
+        load_x(1, 0, PAIR)
         nc.sync.dma_start(out=rows[0:1, D : D + HD], in_=q_norm_w.rearrange("(o k) -> o k", o=1))
         nc.sync.dma_start(out=rows[0:1, D + HD : D + 2 * HD], in_=k_norm_w.rearrange("(o k) -> o k", o=1))
+        load_x(0, PAIR, X_LOAD)
         load_scales(wq_scales, slice(0, Q_HEADS * HD), Wq_scales)
         load_words(wq_words, slice(0, Q_HEADS * HD), Wq_words)
+        load_cos_sin(nc.sync, 0, TABLE_J)
         load_scales(wkv_scales, k_cols, Wk_scales)
         load_scales(wkv_scales, v_cols, Wv_scales)
         load_words(wkv_words, k_cols, Wk_words)
@@ -448,7 +448,7 @@ def tile_rawkvinjector_pa_t_kernel(
         sum_squares(0, slice(0, Q_HEADS))
         normalise_tile(2, 0)
         normalise_tile(2, 1)
-        build_parts("vector", 2)
+        build_parts("vector", 4)
         sum_k_squares_and_copy_v(0)
         multiply(1)
         transpose_pair(2)
@@ -456,7 +456,7 @@ def tile_rawkvinjector_pa_t_kernel(
         regroup(2)
         quantise(1)
         move_norm_weights("gpsimd")
-        build_parts("gpsimd", 5)
+        build_parts("gpsimd", 3)
 
         def pair_with(first, step):
             n = (step - first) // PAIR

@@ -68,7 +68,8 @@ def tile_rawkvinjector_pa_t_kernel(
         ctx.enter_context(tc.manual_schedule())
 
         x_sb = keep.tile([P, BATCH, J, D], BF16)
-        rows = keep.tile([P, D + 2 * HD], BF16)
+        ln_row = keep.tile([P, D], BF16)
+        norm_rows = keep.tile([P, 2 * HD], BF16)
         norm_w = {"vector": keep.tile([P, 2, HD], BF16, name="norm_w_v"), "gpsimd": keep.tile([P, 2, HD], BF16, name="norm_w_g")}
         neg_w = {"vector": keep.tile([P, 2, HALF], BF16, name="neg_w_v"), "gpsimd": keep.tile([P, 2, HALF], BF16, name="neg_w_g")}
         cos_sb = keep.tile([P, J, HD], BF16)
@@ -82,8 +83,9 @@ def tile_rawkvinjector_pa_t_kernel(
         wkv_scales = keep.tile([P, (K_HEADS + V_HEADS) * HD], U8, align_bytes=64)
         one = keep.tile([P, 1], F32)
 
+        nc.gpsimd.memset(ln_row[:].bitcast(F32), 0.0)
         nc.vector.memset(one[:], 1.0)
-        nc.vector.memset(rows[:], 0.0)
+        nc.vector.memset(norm_rows[:], 0.0)
         nc.vector.memset(ones[:], 1.0)
         nc.vector.memset(wq_scales[:].bitcast(I32), 0)
         nc.vector.memset(wkv_scales[:].bitcast(I32), 0)
@@ -117,17 +119,17 @@ def tile_rawkvinjector_pa_t_kernel(
         make_identity(nc, ident[:])
         load_x(0, 0, 1)
         load_x(0, 1, PAIR)
-        nc.sync.dma_start(out=rows[0:1, 0:D], in_=ln1_w.rearrange("(o k) -> o k", o=1))
+        nc.sync.dma_start(out=ln_row[0:1, :], in_=ln1_w.rearrange("(o k) -> o k", o=1))
         load_x(1, 0, PAIR)
-        nc.sync.dma_start(out=rows[0:1, D : D + HD], in_=q_norm_w.rearrange("(o k) -> o k", o=1))
-        nc.sync.dma_start(out=rows[0:1, D + HD : D + 2 * HD], in_=k_norm_w.rearrange("(o k) -> o k", o=1))
+        nc.sync.dma_start(out=norm_rows[0:1, 0:HD], in_=q_norm_w.rearrange("(o k) -> o k", o=1))
+        nc.sync.dma_start(out=norm_rows[0:1, HD : 2 * HD], in_=k_norm_w.rearrange("(o k) -> o k", o=1))
         load_x(0, PAIR, X_LOAD)
         load_scales(wq_scales, slice(0, Q_HEADS * HD), Wq_scales)
         load_words(wq_words, slice(0, Q_HEADS * HD), Wq_words)
         load_cos_sin(nc.sync, 0, TABLE_J)
         load_scales(wkv_scales, k_cols, Wk_scales)
-        load_scales(wkv_scales, v_cols, Wv_scales)
         load_words(wkv_words, k_cols, Wk_words)
+        load_scales(wkv_scales, v_cols, Wv_scales)
         load_words(wkv_words, v_cols, Wv_words)
         load_x(1, PAIR, X_LOAD)
         load_cos_sin(nc.sync, TABLE_J, 2 * TABLE_J)
@@ -139,9 +141,9 @@ def tile_rawkvinjector_pa_t_kernel(
         nc.scalar.activation(out=one[:], in_=one[:], func=ACT.Abs_reciprocal_sqrt)
 
         ln_w = psum_w.tile([P, D], F32)
-        nc.tensor.matmul(out=ln_w[:], lhsT=ones[:], rhs=rows[:, 0:D], start=True, stop=True)
+        nc.tensor.matmul(out=ln_w[:], lhsT=ones[:], rhs=ln_row[:], start=True, stop=True)
         norm_w_ps = psum_u.tile([P, 2 * HD], F32, name="u_q")
-        nc.tensor.matmul(out=norm_w_ps[:], lhsT=ones[:], rhs=rows[:, D : D + 2 * HD], start=True, stop=True)
+        nc.tensor.matmul(out=norm_w_ps[:], lhsT=ones[:], rhs=norm_rows[:], start=True, stop=True)
 
         def move_norm_weights(user):
             if user == "vector":
@@ -263,21 +265,34 @@ def tile_rawkvinjector_pa_t_kernel(
             quantise_tokens(n, 0, PAIR * P)
 
         def multiply(i):
-            tokens = slice((i % PAIR) * P, (i % PAIR + 1) * P)
             u_q = psum_u.tile([P, Q_HEADS * HD], F32)
             u_kv = psum_u.tile([P, (K_HEADS + V_HEADS) * HD], F32)
-            for product, words, scales in ((u_q, wq_words, wq_scales), (u_kv, wkv_words, wkv_scales)):
-                nc.tensor.matmul_mx(
-                    out=product[:],
-                    lhsT=live["h_codes", i // PAIR][:, tokens].bitcast(FP8X4),
-                    lhsT_scale=live["h_scales", i // PAIR][:, tokens],
-                    rhs=words[:].bitcast(FP8X4),
-                    rhs_scale=scales[:],
-                    start=True,
-                    stop=True,
-                )
             live["u_q", i] = u_q
             live["u_kv", i] = u_kv
+            multiply_columns(i, u_q[:], wq_words, wq_scales, slice(0, Q_HEADS * HD))
+            if i < PAIR:
+                multiply_columns(i, u_kv[:, k_cols], wkv_words, wkv_scales, k_cols)
+            else:
+                multiply_columns(i, u_kv[:], wkv_words, wkv_scales, slice(0, (K_HEADS + V_HEADS) * HD))
+                live["u_v", i] = u_kv[:, v_cols]
+
+        def multiply_columns(i, product, words, scales, cols):
+            tokens = slice((i % PAIR) * P, (i % PAIR + 1) * P)
+            nc.tensor.matmul_mx(
+                out=product,
+                lhsT=live["h_codes", i // PAIR][:, tokens].bitcast(FP8X4),
+                lhsT_scale=live["h_scales", i // PAIR][:, tokens],
+                rhs=words[:, cols].bitcast(FP8X4),
+                rhs_scale=scales[:, cols],
+                start=True,
+                stop=True,
+            )
+
+        def multiply_first_v():
+            first_v = psum_u.tile([P, PAIR, V_HEADS * HD], F32, name="u_kv")
+            for i in range(PAIR):
+                multiply_columns(i, first_v[:, i, :], wkv_words, wkv_scales, v_cols)
+                live["u_v", i] = first_v[:, i, :]
 
         def head_of(i, head):
             if head < Q_HEADS:
@@ -298,27 +313,27 @@ def tile_rawkvinjector_pa_t_kernel(
                     accum_out=live["u_sum", i][:, head : head + 1],
                 )
 
-        def sum_k_squares_and_copy_v(i):
+        def copy_v(i):
             jj = i % PAIR
-            sum_squares(i, slice(Q_HEADS, ROPE_HEADS))
             if jj == 0:
                 o_v = stage.tile([P, V_HEADS, PAIR, HD], F32)
                 live["o_v", i // PAIR] = o_v
             o_v = live["o_v", i // PAIR]
-            nc.scalar.copy(
-                out=o_v[:, :, jj, :], in_=live["u_kv", i][:, v_cols].rearrange("p (h d) -> p h d", h=V_HEADS)
-            )
-            u_rstd = small.tile([P, ROPE_HEADS], F32)
-            nc.scalar.activation(out=u_rstd[:], in_=live["u_sum", i][:], func=ACT.Abs_reciprocal_sqrt, scale=1.0 / HD, bias=EPS)
-            live["u_rstd", i] = u_rstd
+            nc.scalar.copy(out=o_v[:, :, jj, :], in_=live["u_v", i].rearrange("p (h d) -> p h d", h=V_HEADS))
             if jj == PAIR - 1:
                 b, j0 = pairs[i // PAIR]
                 queue = nc.scalar if i // PAIR == len(pairs) - 1 else nc.sync
                 queue.dma_start(out=out_2[b].rearrange("h (p j) d -> p h j d", j=J)[:, :, j0 : j0 + PAIR, :], in_=o_v[:])
 
+        def u_rsqrt(i):
+            u_rstd = small.tile([P, ROPE_HEADS], F32)
+            nc.scalar.activation(out=u_rstd[:], in_=live["u_sum", i][:], func=ACT.Abs_reciprocal_sqrt, scale=1.0 / HD, bias=EPS)
+            live["u_rstd", i] = u_rstd
+
         def sum_squares_and_copy_v(i):
-            sum_squares(i, slice(0, Q_HEADS))
-            sum_k_squares_and_copy_v(i)
+            sum_squares(i, slice(0, ROPE_HEADS))
+            copy_v(i)
+            u_rsqrt(i)
 
         def rope_and_store(i):
             b, j0 = pairs[i // PAIR]
@@ -445,14 +460,18 @@ def tile_rawkvinjector_pa_t_kernel(
         multiply(0)
         build_parts("vector", 2)
         regroup(1)
-        sum_squares(0, slice(0, Q_HEADS))
+        sum_squares(0, slice(0, ROPE_HEADS))
         normalise_tile(2, 0)
         normalise_tile(2, 1)
         build_parts("vector", 4)
-        sum_k_squares_and_copy_v(0)
+        u_rsqrt(0)
         multiply(1)
         transpose_pair(2)
-        sum_squares_and_copy_v(1)
+        multiply_first_v()
+        sum_squares(1, slice(0, ROPE_HEADS))
+        copy_v(0)
+        u_rsqrt(1)
+        copy_v(1)
         regroup(2)
         quantise(1)
         move_norm_weights("gpsimd")

@@ -367,16 +367,41 @@ def tile_rawkvinjector_pa_t_kernel(
                     op=ALU.add,
                 )
 
-            def store(dram, heads, jjs):
+            def store(dram, heads, jjs, n=i // PAIR):
+                row, first = pairs[n]
                 nc.sync.dma_start(
-                    out=dram[b].rearrange("h (p j) d -> p h j d", j=J)[:, :, j0 + jjs.start : j0 + jjs.stop, :],
-                    in_=o_qk[:, heads, jjs, :],
+                    out=dram[row].rearrange("h (p j) d -> p h j d", j=J)[:, :, first + jjs.start : first + jjs.stop, :],
+                    in_=live["o_qk", n][:, heads, jjs, :],
                 )
 
+            def add_on_tensor(n, tile_jj):
+                added = psum_t.tile([P, Q_HEADS, 2, HALF], F32, name="h_t")
+                for x in range(2):
+                    for table in range(2):
+                        half = x if table == 0 else 1 - x
+                        nc.tensor.matmul(
+                            out=added[:, :, x, :],
+                            lhsT=ident[:],
+                            rhs=live["products", n][:, table, q_heads, tile_jj, half * HALF : (half + 1) * HALF],
+                            start=table == 0,
+                            stop=table == 1,
+                        )
+                nc.scalar.copy(out=live["o_qk", n][:, q_heads, tile_jj, :], in_=added[:].rearrange("p h x d -> p h (x d)"))
+
             if i // PAIR == len(pairs) - 2:
-                add_tile(nc.gpsimd, slice(0, ROPE_HEADS), jj)
-                store(out_0, q_heads, slice(jj, jj + 1))
-                store(out_1, k_heads, slice(jj, jj + 1))
+                if jj == 0:
+                    add_tile(nc.gpsimd, slice(0, ROPE_HEADS), 0)
+                    store(out_0, q_heads, slice(0, 1))
+                    store(out_1, k_heads, slice(0, 1))
+                else:
+                    add_tile(nc.gpsimd, k_heads, 1)
+                    store(out_1, k_heads, slice(1, PAIR))
+            elif i // PAIR >= len(pairs) - 3  and i // PAIR < len(pairs) - 1:
+                if jj == PAIR - 1:
+                    for tile_jj in reversed(range(PAIR)):
+                        add_tile(nc.gpsimd, slice(0, ROPE_HEADS), tile_jj)
+                        store(out_0, q_heads, slice(tile_jj, tile_jj + 1))
+                        store(out_1, k_heads, slice(tile_jj, tile_jj + 1))
             elif i // PAIR < len(pairs) - 1:
                 if jj == PAIR - 1:
                     nc.gpsimd.tensor_tensor(
@@ -387,13 +412,16 @@ def tile_rawkvinjector_pa_t_kernel(
                     )
                     store(out_0, q_heads, slice(0, PAIR))
                     store(out_1, k_heads, slice(0, PAIR))
-            elif jj == PAIR - 1:
+            elif jj == 0:
+                add_on_tensor(i // PAIR - 1, 1)
+                store(out_0, q_heads, slice(1, PAIR), i // PAIR - 1)
+                add_tile(nc.gpsimd, k_heads, 0)
+                store(out_1, k_heads, slice(0, 1))
+            else:
                 add_tile(nc.vector, q_heads, 0)
                 store(out_0, q_heads, slice(0, 1))
                 add_tile(nc.vector, q_heads, 1)
                 store(out_0, q_heads, slice(1, PAIR))
-                add_tile(nc.vector, k_heads, 0)
-                store(out_1, k_heads, slice(0, 1))
                 add_tile(nc.vector, k_heads, 1)
                 store(out_1, k_heads, slice(1, PAIR))
 

@@ -36,6 +36,7 @@ LAG_REGROUP = 2
 RUN_AHEAD = 2
 LAG_MATMUL = 3
 LAG_SQUARES = 4
+PE_HEADS = 2
 LAG_ROPE = 5
 
 
@@ -70,7 +71,7 @@ def tile_rawkvinjector_pa_t_kernel(
         x_sb = keep.tile([P, BATCH, J, D], BF16)
         ln_row = keep.tile([P, D], BF16)
         norm_rows = keep.tile([P, 2 * HD], BF16)
-        norm_w = {"vector": keep.tile([P, 2, HD], BF16, name="norm_w_v"), "gpsimd": keep.tile([P, 2, HD], BF16, name="norm_w_g")}
+        norm_w = keep.tile([P, 2, HD], BF16)
         neg_w = {"vector": keep.tile([P, 2, HALF], BF16, name="neg_w_v"), "gpsimd": keep.tile([P, 2, HALF], BF16, name="neg_w_g")}
         cos_sb = keep.tile([P, J, HD], BF16)
         sin_sb = keep.tile([P, J, HD], BF16)
@@ -145,13 +146,12 @@ def tile_rawkvinjector_pa_t_kernel(
         norm_w_ps = psum_u.tile([P, 2 * HD], F32, name="u_q")
         nc.tensor.matmul(out=norm_w_ps[:], lhsT=ones[:], rhs=norm_rows[:], start=True, stop=True)
 
-        def move_norm_weights(user):
-            if user == "vector":
-                nc.vector.tensor_copy(out=norm_w[user][:].rearrange("p a d -> p (a d)"), in_=norm_w_ps[:])
-            else:
-                nc.vector.tensor_copy(out=norm_w[user][:], in_=norm_w["vector"][:])
+        def move_norm_weights():
+            nc.vector.tensor_copy(out=norm_w[:].rearrange("p a d -> p (a d)"), in_=norm_w_ps[:])
+
+        def negate_norm_weights(user):
             nc.vector.tensor_scalar(
-                out=neg_w[user][:], in0=norm_w["vector"][:, :, HALF:HD], scalar1=-1.0, scalar2=0.0, op0=ALU.mult, op1=ALU.add
+                out=neg_w[user][:], in0=norm_w[:, :, HALF:HD], scalar1=-1.0, scalar2=0.0, op0=ALU.mult, op1=ALU.add
             )
 
         def build_table_part(user, j0, j1, table, half):
@@ -159,7 +159,7 @@ def tile_rawkvinjector_pa_t_kernel(
             here = slice(half * HALF, (half + 1) * HALF)
             other = slice((1 - half) * HALF, (2 - half) * HALF)
             trig = cos_sb[:, js, here] if table == 0 else sin_sb[:, js, other]
-            weight = neg_w[user][:] if (table, half) == (1, 1) else norm_w[user][:, :, here]
+            weight = neg_w[user][:] if (table, half) == (1, 1) else norm_w[:, :, here]
             engine = nc.vector if user == "vector" else nc.gpsimd
             engine.tensor_tensor(
                 out=tables[:, :, js, table, here],
@@ -374,19 +374,19 @@ def tile_rawkvinjector_pa_t_kernel(
                     in_=live["o_qk", n][:, heads, jjs, :],
                 )
 
-            def add_on_tensor(n, tile_jj):
-                added = psum_t.tile([P, Q_HEADS, 2, HALF], F32, name="h_t")
+            def add_on_tensor(n, tile_jj, heads, pool, bank):
+                added = pool.tile([P, heads.stop - heads.start, 2, HALF], F32, name=bank)
                 for x in range(2):
                     for table in range(2):
                         half = x if table == 0 else 1 - x
                         nc.tensor.matmul(
                             out=added[:, :, x, :],
                             lhsT=ident[:],
-                            rhs=live["products", n][:, table, q_heads, tile_jj, half * HALF : (half + 1) * HALF],
+                            rhs=live["products", n][:, table, heads, tile_jj, half * HALF : (half + 1) * HALF],
                             start=table == 0,
                             stop=table == 1,
                         )
-                nc.scalar.copy(out=live["o_qk", n][:, q_heads, tile_jj, :], in_=added[:].rearrange("p h x d -> p h (x d)"))
+                nc.scalar.copy(out=live["o_qk", n][:, heads, tile_jj, :], in_=added[:].rearrange("p h x d -> p h (x d)"))
 
             if i // PAIR == len(pairs) - 2:
                 if jj == 0:
@@ -413,12 +413,13 @@ def tile_rawkvinjector_pa_t_kernel(
                     store(out_0, q_heads, slice(0, PAIR))
                     store(out_1, k_heads, slice(0, PAIR))
             elif jj == 0:
-                add_on_tensor(i // PAIR - 1, 1)
+                add_on_tensor(i // PAIR - 1, 1, q_heads, psum_t, "h_t")
+                add_on_tensor(i // PAIR, 0, slice(0, PE_HEADS), psum_u, "u_q")
                 store(out_0, q_heads, slice(1, PAIR), i // PAIR - 1)
                 add_tile(nc.gpsimd, k_heads, 0)
                 store(out_1, k_heads, slice(0, 1))
             else:
-                add_tile(nc.vector, q_heads, 0)
+                add_tile(nc.vector, slice(PE_HEADS, Q_HEADS), 0)
                 store(out_0, q_heads, slice(0, 1))
                 add_tile(nc.vector, q_heads, 1)
                 store(out_0, q_heads, slice(1, PAIR))
@@ -452,14 +453,10 @@ def tile_rawkvinjector_pa_t_kernel(
                 one_stage(index)
 
         chunks = [(0, PAIR), (PAIR, TABLE_J)] + [(j0, j0 + TABLE_J) for j0 in range(TABLE_J, J, TABLE_J)]
-        parts = [(j0, j1, table, half) for j0, j1 in chunks for table in range(2) for half in range(2)]
-        built = {"parts": 0}
-
-        def build_parts(user, count):
-            for part in range(count):
-                j0, j1, table, half = parts[built["parts"]]
-                built["parts"] = built["parts"] + 1
-                build_table_part(user, j0, j1, table, half)
+        parts = [(j0, j1, table, half) for j0, j1 in chunks for table, half in ((0, 0), (0, 1), (1, 1), (1, 0))]
+        def build_parts(user, numbers):
+            for number in numbers:
+                build_table_part(user, *parts[number])
 
         for jj in range(PAIR):
             sum_x_squares_of_tile(0, jj)
@@ -470,7 +467,8 @@ def tile_rawkvinjector_pa_t_kernel(
         sum_x_squares(1)
         x_rsqrt(1)
         normalise_tile(0, 1)
-        move_norm_weights("vector")
+        move_norm_weights()
+        negate_norm_weights("vector")
         second_t = psum_t.tile([P, 2, P], F32, name="h_t")
         transpose_tile(0, 1, lambda u: second_t[:, u, :])
         new_grouped(0)
@@ -485,13 +483,15 @@ def tile_rawkvinjector_pa_t_kernel(
         sum_x_squares_of_tile(2, 1)
         x_rsqrt(2)
         quantise_tokens(0, P, PAIR * P)
+        negate_norm_weights("gpsimd")
+        build_parts("gpsimd", (2, 3))
         multiply(0)
-        build_parts("vector", 2)
         regroup(1)
         sum_squares(0, slice(0, ROPE_HEADS))
         normalise_tile(2, 0)
         normalise_tile(2, 1)
-        build_parts("vector", 4)
+        quantise(1)
+        build_parts("vector", (0, 1, 4, 5))
         u_rsqrt(0)
         multiply(1)
         transpose_pair(2)
@@ -501,9 +501,8 @@ def tile_rawkvinjector_pa_t_kernel(
         u_rsqrt(1)
         copy_v(1)
         regroup(2)
-        quantise(1)
-        move_norm_weights("gpsimd")
-        build_parts("gpsimd", 3)
+        negate_norm_weights("gpsimd")
+        build_parts("gpsimd", (6, 7, 8))
 
         def pair_with(first, step):
             n = (step - first) // PAIR
@@ -519,8 +518,8 @@ def tile_rawkvinjector_pa_t_kernel(
                 run(sum_squares_and_copy_v, tile_at(step, LAG_SQUARES))
             run(rope_and_store, tile_at(step, LAG_ROPE))
             summed = pair_at(step, LAG_ROPE + PAIR - 1)
-            if summed is not None and built["parts"] < len(parts):
-                build_parts("gpsimd", 1)
+            if summed is not None and 9 + summed < len(parts):
+                build_parts("gpsimd", (9 + summed,))
             run(sum_x_squares, pair_with(-1, step))
             run(x_rsqrt, pair_with(-1, step))
             run(regroup, pair_with(1, step))

@@ -37,6 +37,7 @@ RUN_AHEAD = 2
 LAG_MATMUL = 3
 LAG_SQUARES = 4
 PE_HEADS = 2
+EARLY_HEADS = 2
 LAG_ROPE = 5
 
 
@@ -369,8 +370,11 @@ def tile_rawkvinjector_pa_t_kernel(
 
             def store(dram, heads, jjs, n=i // PAIR):
                 row, first = pairs[n]
+                first_head = 0 if dram is out_0 else Q_HEADS
                 nc.sync.dma_start(
-                    out=dram[row].rearrange("h (p j) d -> p h j d", j=J)[:, :, first + jjs.start : first + jjs.stop, :],
+                    out=dram[row, heads.start - first_head : heads.stop - first_head].rearrange("h (p j) d -> p h j d", j=J)[
+                        :, :, first + jjs.start : first + jjs.stop, :
+                    ],
                     in_=live["o_qk", n][:, heads, jjs, :],
                 )
 
@@ -397,11 +401,17 @@ def tile_rawkvinjector_pa_t_kernel(
                     add_tile(nc.gpsimd, k_heads, 1)
                     store(out_1, k_heads, slice(1, PAIR))
             elif i // PAIR >= len(pairs) - 3  and i // PAIR < len(pairs) - 1:
-                if jj == PAIR - 1:
-                    for tile_jj in reversed(range(PAIR)):
-                        add_tile(nc.gpsimd, slice(0, ROPE_HEADS), tile_jj)
-                        store(out_0, q_heads, slice(tile_jj, tile_jj + 1))
-                        store(out_1, k_heads, slice(tile_jj, tile_jj + 1))
+                early = slice(0, EARLY_HEADS)
+                if jj == 0:
+                    add_tile(nc.gpsimd, early, 0)
+                    store(out_0, early, slice(0, 1))
+                else:
+                    add_tile(nc.gpsimd, slice(0, ROPE_HEADS), 1)
+                    store(out_0, q_heads, slice(1, PAIR))
+                    store(out_1, k_heads, slice(1, PAIR))
+                    add_tile(nc.gpsimd, slice(EARLY_HEADS, ROPE_HEADS), 0)
+                    store(out_0, slice(EARLY_HEADS, Q_HEADS), slice(0, 1))
+                    store(out_1, k_heads, slice(0, 1))
             elif i // PAIR < len(pairs) - 1:
                 if jj == PAIR - 1:
                     nc.gpsimd.tensor_tensor(

from contextlib import ExitStack

import concourse.mybir as mybir
from concourse.masks import make_identity

F32 = mybir.dt.float32
BF16 = mybir.dt.bfloat16
I32 = mybir.dt.int32
U8 = mybir.dt.uint8
U32 = mybir.dt.uint32
FP8X4 = mybir.dt.float8_e4m3fn_x4
ACT = mybir.ActivationFunctionType
ALU = mybir.AluOpType

P = 128
BATCH = 2
T = 2048
D = 512
HD = 128
HALF = HD // 2
Q_HEADS = 4
K_HEADS = 2
V_HEADS = 2
ROPE_HEADS = Q_HEADS + K_HEADS
J = T // P
PAIR = 2
X_LOAD = 4
TABLE_J = 4
EPS = 1e-6
SCALE_ROWS = 4

FLOPS = 2 * BATCH * T * D * (Q_HEADS + K_HEADS + V_HEADS) * HD

LAG_H = 1
LAG_REGROUP = 2
RUN_AHEAD = 2
LAG_MATMUL = 3
LAG_SQUARES = 4
PE_HEADS = 2
EARLY_HEADS = 2
LAG_ROPE = 5


def tile_rawkvinjector_pa_t_kernel(
    tc,
    hidden_states,
    ln1_w,
    Wq_words,
    Wq_scales,
    Wk_words,
    Wk_scales,
    Wv_words,
    Wv_scales,
    q_norm_w,
    k_norm_w,
    cos,
    sin,
    out_0,
    out_1,
    out_2,
):
    nc = tc.nc
    with ExitStack() as ctx:
        keep = ctx.enter_context(tc.tile_pool(name="keep", bufs=1))
        small = ctx.enter_context(tc.tile_pool(name="small", bufs=4))
        stage = ctx.enter_context(tc.tile_pool(name="stage", bufs=3))
        psum_w = ctx.enter_context(tc.psum_pool(name="psum_w", bufs=1))
        psum_t = ctx.enter_context(tc.psum_pool(name="psum_t", bufs=1))
        psum_u = ctx.enter_context(tc.psum_pool(name="psum_u", bufs=3))
        ctx.enter_context(tc.manual_schedule())

        x_sb = keep.tile([P, BATCH, J, D], BF16)
        ln_row = keep.tile([P, D], BF16)
        norm_rows = keep.tile([P, 2 * HD], BF16)
        norm_w = keep.tile([P, 2, HD], BF16)
        neg_w = {"vector": keep.tile([P, 2, HALF], BF16, name="neg_w_v"), "gpsimd": keep.tile([P, 2, HALF], BF16, name="neg_w_g")}
        cos_sb = keep.tile([P, J, HD], BF16)
        sin_sb = keep.tile([P, J, HD], BF16)
        tables = keep.tile([P, 2, J, 2, HD], F32)
        ident = keep.tile([P, P], F32)
        ones = keep.tile([P, P], BF16)
        wq_words = keep.tile([P, Q_HEADS * HD], U32, align_bytes=64)
        wkv_words = keep.tile([P, (K_HEADS + V_HEADS) * HD], U32, align_bytes=64)
        wq_scales = keep.tile([P, Q_HEADS * HD], U8, align_bytes=64)
        wkv_scales = keep.tile([P, (K_HEADS + V_HEADS) * HD], U8, align_bytes=64)
        one = keep.tile([P, 1], F32)

        nc.gpsimd.memset(ln_row[:].bitcast(F32), 0.0)
        nc.vector.memset(one[:], 1.0)
        nc.vector.memset(norm_rows[:], 0.0)
        nc.vector.memset(ones[:], 1.0)
        nc.vector.memset(wq_scales[:].bitcast(I32), 0)
        nc.vector.memset(wkv_scales[:].bitcast(I32), 0)

        x_dram = hidden_states.rearrange("b (p j) k -> p b j k", j=J)

        def load_x(b, j0, j1, queue=nc.sync):
            queue.dma_start(out=x_sb[:, b, j0:j1, :], in_=x_dram[:, b, j0:j1, :])

        def load_scales(plane, cols, scales):
            for quadrant in range(P // 32):
                rows = slice(SCALE_ROWS * quadrant, SCALE_ROWS * (quadrant + 1))
                parts = slice(32 * quadrant, 32 * quadrant + SCALE_ROWS)
                nc.sync.dma_start(out=plane[parts, cols].bitcast(I32), in_=scales[0, rows, :].bitcast(I32))

        def load_words(words, cols, packed):
            nc.sync.dma_start(
                out=words[:, cols].bitcast(I32),
                in_=packed[0].rearrange("p n t -> p (n t)").bitcast(I32),
            )

        k_cols = slice(0, K_HEADS * HD)
        v_cols = slice(K_HEADS * HD, (K_HEADS + V_HEADS) * HD)
        cos_dram = cos.rearrange("(p j) d -> p j d", j=J)
        sin_dram = sin.rearrange("(p j) d -> p j d", j=J)

        def load_cos_sin(queue, j0, j1):
            queue.dma_start(out=cos_sb[:, j0:j1, :], in_=cos_dram[:, j0:j1, :])
            queue.dma_start(out=sin_sb[:, j0:j1, :], in_=sin_dram[:, j0:j1, :])

        make_identity(nc, ident[:])
        load_x(0, 0, 1)
        load_x(0, 1, PAIR)
        nc.sync.dma_start(out=ln_row[0:1, :], in_=ln1_w.rearrange("(o k) -> o k", o=1))
        load_x(1, 0, PAIR)
        nc.sync.dma_start(out=norm_rows[0:1, 0:HD], in_=q_norm_w.rearrange("(o k) -> o k", o=1))
        nc.sync.dma_start(out=norm_rows[0:1, HD : 2 * HD], in_=k_norm_w.rearrange("(o k) -> o k", o=1))
        load_x(0, PAIR, X_LOAD)
        load_scales(wq_scales, slice(0, Q_HEADS * HD), Wq_scales)
        load_words(wq_words, slice(0, Q_HEADS * HD), Wq_words)
        load_cos_sin(nc.sync, 0, TABLE_J)
        load_scales(wkv_scales, k_cols, Wk_scales)
        load_words(wkv_words, k_cols, Wk_words)
        load_scales(wkv_scales, v_cols, Wv_scales)
        load_words(wkv_words, v_cols, Wv_words)
        load_x(1, PAIR, X_LOAD)
        load_cos_sin(nc.sync, TABLE_J, 2 * TABLE_J)
        load_cos_sin(nc.sync, 2 * TABLE_J, J)
        for j0 in range(X_LOAD, J, X_LOAD):
            for b in range(BATCH):
                load_x(b, j0, j0 + X_LOAD)

        nc.scalar.activation(out=one[:], in_=one[:], func=ACT.Abs_reciprocal_sqrt)

        ln_w = psum_w.tile([P, D], F32)
        nc.tensor.matmul(out=ln_w[:], lhsT=ones[:], rhs=ln_row[:], start=True, stop=True)
        norm_w_ps = psum_u.tile([P, 2 * HD], F32, name="u_q")
        nc.tensor.matmul(out=norm_w_ps[:], lhsT=ones[:], rhs=norm_rows[:], start=True, stop=True)

        def move_norm_weights():
            nc.vector.tensor_copy(out=norm_w[:].rearrange("p a d -> p (a d)"), in_=norm_w_ps[:])

        def negate_norm_weights(user):
            nc.vector.tensor_scalar(
                out=neg_w[user][:], in0=norm_w[:, :, HALF:HD], scalar1=-1.0, scalar2=0.0, op0=ALU.mult, op1=ALU.add
            )

        def build_table_part(user, j0, j1, table, half):
            js = slice(j0, j1)
            here = slice(half * HALF, (half + 1) * HALF)
            other = slice((1 - half) * HALF, (2 - half) * HALF)
            trig = cos_sb[:, js, here] if table == 0 else sin_sb[:, js, other]
            weight = neg_w[user][:] if (table, half) == (1, 1) else norm_w[:, :, here]
            engine = nc.vector if user == "vector" else nc.gpsimd
            engine.tensor_tensor(
                out=tables[:, :, js, table, here],
                in0=trig.unsqueeze(1).to_broadcast([P, 2, j1 - j0, HALF]),
                in1=weight.unsqueeze(2).to_broadcast([P, 2, j1 - j0, HALF]),
                op=ALU.mult,
            )

        pairs = [(b, j0) for j0 in range(0, J, PAIR) for b in range(BATCH)]
        live = {}

        def sum_x_squares_of_tile(n, jj):
            b, j0 = pairs[n]
            if jj == 0:
                x_squares = stage.tile([P, PAIR, D], BF16)
                x_sum = small.tile([P, PAIR], F32)
                x_rstd = small.tile([P, PAIR], F32)
                live["x_squares", n] = x_squares
                live["x_sum", n] = x_sum
                live["x_rstd", n] = x_rstd
            nc.scalar.activation(
                out=live["x_squares", n][:, jj, :],
                in_=x_sb[:, b, j0 + jj, :],
                func=ACT.Square,
                accum_out=live["x_sum", n][:, jj : jj + 1],
            )

        def sum_x_squares(n):
            for jj in range(PAIR):
                sum_x_squares_of_tile(n, jj)

        def x_rsqrt_columns(n, jjs):
            nc.scalar.activation(
                out=live["x_rstd", n][:, jjs],
                in_=live["x_sum", n][:, jjs],
                func=ACT.Abs_reciprocal_sqrt,
                scale=1.0 / D,
                bias=EPS,
            )

        def x_rsqrt(n):
            x_rsqrt_columns(n, slice(0, PAIR))

        def normalise_tile(n, jj):
            b, j0 = pairs[n]
            if jj == 0:
                h = stage.tile([P, PAIR, D], BF16)
                live["h", n] = h
            nc.vector.scalar_tensor_tensor(
                out=live["h", n][:, jj, :],
                in0=x_sb[:, b, j0 + jj, :],
                scalar=live["x_rstd", n][:, jj : jj + 1],
                in1=ln_w[:],
                op0=ALU.mult,
                op1=ALU.mult,
            )

        def transpose_tile(n, jj, plane_out):
            h_words = live["h", n][:, jj, :].bitcast(F32)
            for u in range(2):
                nc.tensor.transpose(plane_out(u), h_words[:, u : D // 2 : 2], ident[:])

        def normalise_and_transpose(n):
            for jj in range(PAIR):
                normalise_tile(n, jj)
            transpose_pair(n)

        def transpose_pair(n):
            h_t = psum_t.tile([P, 2, PAIR * P], F32)
            for jj in range(PAIR):
                transpose_tile(n, jj, lambda u: h_t[:, u, jj * P : (jj + 1) * P])
            live["h_t", n] = h_t

        def new_grouped(n):
            grouped = stage.tile([P, PAIR * P * 4], BF16, align_bytes=64)
            live["grouped", n] = grouped

        def regroup_words(n, tokens, planes):
            nc.scalar.copy(
                out=live["grouped", n][:].bitcast(F32).rearrange("p (r u) -> p r u", u=2)[:, tokens, :],
                in_=planes.rearrange("p u r -> p r u"),
            )

        def regroup(n):
            new_grouped(n)
            regroup_words(n, slice(0, PAIR * P), live["h_t", n][:])

        def new_codes(n):
            h_codes = stage.tile([P, PAIR * P], U32, align_bytes=64)
            h_scales = stage.tile([P, PAIR * P], U8, align_bytes=64)
            live["h_codes", n] = h_codes
            live["h_scales", n] = h_scales

        def quantise_tokens(n, t0, t1):
            nc.vector.quantize_mx(
                out=live["h_codes", n][:, t0:t1].bitcast(FP8X4),
                scales=live["h_scales", n][:, t0:t1],
                in_=live["grouped", n][:, 4 * t0 : 4 * t1],
            )

        def quantise(n):
            new_codes(n)
            quantise_tokens(n, 0, PAIR * P)

        def multiply(i):
            u_q = psum_u.tile([P, Q_HEADS * HD], F32)
            u_kv = psum_u.tile([P, (K_HEADS + V_HEADS) * HD], F32)
            live["u_q", i] = u_q
            live["u_kv", i] = u_kv
            multiply_columns(i, u_q[:], wq_words, wq_scales, slice(0, Q_HEADS * HD))
            if i < PAIR:
                multiply_columns(i, u_kv[:, k_cols], wkv_words, wkv_scales, k_cols)
            else:
                multiply_columns(i, u_kv[:], wkv_words, wkv_scales, slice(0, (K_HEADS + V_HEADS) * HD))
                live["u_v", i] = u_kv[:, v_cols]

        def multiply_columns(i, product, words, scales, cols):
            tokens = slice((i % PAIR) * P, (i % PAIR + 1) * P)
            nc.tensor.matmul_mx(
                out=product,
                lhsT=live["h_codes", i // PAIR][:, tokens].bitcast(FP8X4),
                lhsT_scale=live["h_scales", i // PAIR][:, tokens],
                rhs=words[:, cols].bitcast(FP8X4),
                rhs_scale=scales[:, cols],
                start=True,
                stop=True,
            )

        def multiply_first_v():
            first_v = psum_u.tile([P, PAIR, V_HEADS * HD], F32, name="u_kv")
            for i in range(PAIR):
                multiply_columns(i, first_v[:, i, :], wkv_words, wkv_scales, v_cols)
                live["u_v", i] = first_v[:, i, :]

        def head_of(i, head):
            if head < Q_HEADS:
                return live["u_q", i][:, head * HD : (head + 1) * HD]
            return live["u_kv", i][:, (head - Q_HEADS) * HD : (head - Q_HEADS + 1) * HD]

        def sum_squares(i, heads):
            if heads.start == 0:
                u_squares = stage.tile([P, ROPE_HEADS, HD], BF16)
                u_sum = small.tile([P, ROPE_HEADS], F32)
                live["u_squares", i] = u_squares
                live["u_sum", i] = u_sum
            for head in range(heads.start, heads.stop):
                nc.scalar.activation(
                    out=live["u_squares", i][:, head, :],
                    in_=head_of(i, head),
                    func=ACT.Square,
                    accum_out=live["u_sum", i][:, head : head + 1],
                )

        def copy_v(i):
            jj = i % PAIR
            if jj == 0:
                o_v = stage.tile([P, V_HEADS, PAIR, HD], F32)
                live["o_v", i // PAIR] = o_v
            o_v = live["o_v", i // PAIR]
            nc.scalar.copy(out=o_v[:, :, jj, :], in_=live["u_v", i].rearrange("p (h d) -> p h d", h=V_HEADS))
            if jj == PAIR - 1:
                b, j0 = pairs[i // PAIR]
                queue = nc.scalar if i // PAIR == len(pairs) - 1 else nc.sync
                queue.dma_start(out=out_2[b].rearrange("h (p j) d -> p h j d", j=J)[:, :, j0 : j0 + PAIR, :], in_=o_v[:])

        def u_rsqrt(i):
            u_rstd = small.tile([P, ROPE_HEADS], F32)
            nc.scalar.activation(out=u_rstd[:], in_=live["u_sum", i][:], func=ACT.Abs_reciprocal_sqrt, scale=1.0 / HD, bias=EPS)
            live["u_rstd", i] = u_rstd

        def sum_squares_and_copy_v(i):
            sum_squares(i, slice(0, ROPE_HEADS))
            copy_v(i)
            u_rsqrt(i)

        def rope_and_store(i):
            b, j0 = pairs[i // PAIR]
            jj = i % PAIR
            u_rstd = live["u_rstd", i]
            if jj == 0:
                products = stage.tile([P, 2, ROPE_HEADS, PAIR, HD], F32)
                live["products", i // PAIR] = products
            products = live["products", i // PAIR]
            for head in range(ROPE_HEADS):
                q_or_k = 0 if head < Q_HEADS else 1
                nc.vector.scalar_tensor_tensor(
                    out=products[:, :, head, jj, :],
                    in0=head_of(i, head).unsqueeze(1).to_broadcast([P, 2, HD]),
                    scalar=u_rstd[:, head : head + 1],
                    in1=tables[:, q_or_k, j0 + jj, :, :],
                    op0=ALU.mult,
                    op1=ALU.mult,
                )
            if jj == 0:
                o_qk = stage.tile([P, ROPE_HEADS, PAIR, HD], F32)
                live["o_qk", i // PAIR] = o_qk
            o_qk = live["o_qk", i // PAIR]
            q_heads, k_heads = slice(0, Q_HEADS), slice(Q_HEADS, ROPE_HEADS)

            def add_tile(engine, heads, tile_jj):
                engine.tensor_tensor(
                    out=o_qk[:, heads, tile_jj, :].rearrange("p h (x d) -> p h x d", x=2),
                    in0=products[:, 0, heads, tile_jj, :].rearrange("p h (x d) -> p h x d", x=2),
                    in1=products[:, 1, heads, tile_jj, :].rearrange("p h (x d) -> p h x d", x=2)[:, :, ::-1, :],
                    op=ALU.add,
                )

            def store(dram, heads, jjs, n=i // PAIR):
                row, first = pairs[n]
                first_head = 0 if dram is out_0 else Q_HEADS
                nc.sync.dma_start(
                    out=dram[row, heads.start - first_head : heads.stop - first_head].rearrange("h (p j) d -> p h j d", j=J)[
                        :, :, first + jjs.start : first + jjs.stop, :
                    ],
                    in_=live["o_qk", n][:, heads, jjs, :],
                )

            def add_on_tensor(n, tile_jj, heads, pool, bank):
                added = pool.tile([P, heads.stop - heads.start, 2, HALF], F32, name=bank)
                for x in range(2):
                    for table in range(2):
                        half = x if table == 0 else 1 - x
                        nc.tensor.matmul(
                            out=added[:, :, x, :],
                            lhsT=ident[:],
                            rhs=live["products", n][:, table, heads, tile_jj, half * HALF : (half + 1) * HALF],
                            start=table == 0,
                            stop=table == 1,
                        )
                nc.scalar.copy(out=live["o_qk", n][:, heads, tile_jj, :], in_=added[:].rearrange("p h x d -> p h (x d)"))

            if i // PAIR == len(pairs) - 2:
                if jj == 0:
                    add_tile(nc.gpsimd, slice(0, ROPE_HEADS), 0)
                    store(out_0, q_heads, slice(0, 1))
                    store(out_1, k_heads, slice(0, 1))
                else:
                    add_tile(nc.gpsimd, k_heads, 1)
                    store(out_1, k_heads, slice(1, PAIR))
            elif i // PAIR >= len(pairs) - 3  and i // PAIR < len(pairs) - 1:
                early = slice(0, EARLY_HEADS)
                if jj == 0:
                    add_tile(nc.gpsimd, early, 0)
                    store(out_0, early, slice(0, 1))
                else:
                    add_tile(nc.gpsimd, slice(0, ROPE_HEADS), 1)
                    store(out_0, q_heads, slice(1, PAIR))
                    store(out_1, k_heads, slice(1, PAIR))
                    add_tile(nc.gpsimd, slice(EARLY_HEADS, ROPE_HEADS), 0)
                    store(out_0, slice(EARLY_HEADS, Q_HEADS), slice(0, 1))
                    store(out_1, k_heads, slice(0, 1))
            elif i // PAIR < len(pairs) - 1:
                if jj == PAIR - 1:
                    nc.gpsimd.tensor_tensor(
                        out=o_qk[:].rearrange("p h j (x d) -> p (h j) x d", x=2),
                        in0=products[:, 0, :, :, :].rearrange("p h j (x d) -> p (h j) x d", x=2),
                        in1=products[:, 1, :, :, :].rearrange("p h j (x d) -> p (h j) x d", x=2)[:, :, ::-1, :],
                        op=ALU.add,
                    )
                    store(out_0, q_heads, slice(0, PAIR))
                    store(out_1, k_heads, slice(0, PAIR))
            elif jj == 0:
                add_on_tensor(i // PAIR - 1, 1, q_heads, psum_t, "h_t")
                add_on_tensor(i // PAIR, 0, slice(0, PE_HEADS), psum_u, "u_q")
                store(out_0, q_heads, slice(1, PAIR), i // PAIR - 1)
                add_tile(nc.gpsimd, k_heads, 0)
                store(out_1, k_heads, slice(0, 1))
            else:
                add_tile(nc.vector, slice(PE_HEADS, Q_HEADS), 0)
                store(out_0, q_heads, slice(0, 1))
                add_tile(nc.vector, q_heads, 1)
                store(out_0, q_heads, slice(1, PAIR))
                add_tile(nc.vector, k_heads, 1)
                store(out_1, k_heads, slice(1, PAIR))

        def pair_at(step, lag):
            first = step - lag
            if first % PAIR == 0 and 0 <= first // PAIR < len(pairs):
                return first // PAIR
            return None

        def front_start(n):
            return max(n, PAIR * n - RUN_AHEAD)

        def front_at(step, lag):
            found = [n for n in range(len(pairs)) if front_start(n) + lag == step]
            return found[0] if found else None

        def tile_at(step, lag):
            return step - lag if 0 <= step - lag < PAIR * len(pairs) else None

        done = set()

        def start(one_stage, index):
            one_stage(index)
            done.add((one_stage, index))

        def run(one_stage, index):
            if index is not None and (one_stage, index) not in done:
                one_stage(index)

        chunks = [(0, PAIR), (PAIR, TABLE_J)] + [(j0, j0 + TABLE_J) for j0 in range(TABLE_J, J, TABLE_J)]
        parts = [(j0, j1, table, half) for j0, j1 in chunks for table, half in ((0, 0), (0, 1), (1, 1), (1, 0))]
        def build_parts(user, numbers):
            for number in numbers:
                build_table_part(user, *parts[number])

        for jj in range(PAIR):
            sum_x_squares_of_tile(0, jj)
            x_rsqrt_columns(0, slice(jj, jj + 1))
        normalise_tile(0, 0)
        first_t = psum_u.tile([P, 2, P], F32, name="u_q")
        transpose_tile(0, 0, lambda u: first_t[:, u, :])
        sum_x_squares(1)
        x_rsqrt(1)
        normalise_tile(0, 1)
        move_norm_weights()
        negate_norm_weights("vector")
        second_t = psum_t.tile([P, 2, P], F32, name="h_t")
        transpose_tile(0, 1, lambda u: second_t[:, u, :])
        new_grouped(0)
        new_codes(0)
        regroup_words(0, slice(0, P), first_t[:])
        normalise_tile(1, 0)
        quantise_tokens(0, 0, P)
        sum_x_squares_of_tile(2, 0)
        normalise_tile(1, 1)
        regroup_words(0, slice(P, PAIR * P), second_t[:])
        transpose_pair(1)
        sum_x_squares_of_tile(2, 1)
        x_rsqrt(2)
        quantise_tokens(0, P, PAIR * P)
        negate_norm_weights("gpsimd")
        build_parts("gpsimd", (2, 3))
        multiply(0)
        regroup(1)
        sum_squares(0, slice(0, ROPE_HEADS))
        normalise_tile(2, 0)
        normalise_tile(2, 1)
        quantise(1)
        build_parts("vector", (0, 1, 4, 5))
        u_rsqrt(0)
        multiply(1)
        transpose_pair(2)
        multiply_first_v()
        sum_squares(1, slice(0, ROPE_HEADS))
        copy_v(0)
        u_rsqrt(1)
        copy_v(1)
        regroup(2)
        negate_norm_weights("gpsimd")
        build_parts("gpsimd", (6, 7, 8))

        def pair_with(first, step):
            n = (step - first) // PAIR
            return n if (step - first) % PAIR == 0 and 3 <= n < len(pairs) else None

        for step in range(4, PAIR * len(pairs) + LAG_ROPE):
            if step > LAG_MATMUL + PAIR:
                run(quantise, pair_at(step, LAG_MATMUL))
            if step > LAG_MATMUL + 1:
                run(multiply, tile_at(step, LAG_MATMUL))
            run(normalise_and_transpose, pair_with(1, step))
            if step > LAG_SQUARES + 1:
                run(sum_squares_and_copy_v, tile_at(step, LAG_SQUARES))
            run(rope_and_store, tile_at(step, LAG_ROPE))
            summed = pair_at(step, LAG_ROPE + PAIR - 1)
            if summed is not None and 9 + summed < len(parts):
                build_parts("gpsimd", (9 + summed,))
            run(sum_x_squares, pair_with(-1, step))
            run(x_rsqrt, pair_with(-1, step))
            run(regroup, pair_with(1, step))
